import numpy as np
import ml_dtypes


def mxq(x, axis, fmt="e4m3"):
    dtype, down = {"e4m3": (ml_dtypes.float8_e4m3fn, 7), "e5m2": (ml_dtypes.float8_e5m2, 14)}[fmt]
    v = np.moveaxis(np.asarray(x, np.float32).astype(ml_dtypes.bfloat16).astype(np.float64), axis, -1)
    blocks = v.reshape(v.shape[:-1] + (-1, 32))
    amax = np.abs(blocks).max(-1, keepdims=True)
    byte = np.maximum(np.where(amax > 0, np.frexp(amax)[1] - 1 + 127, 0) - down, 1)
    scale = np.exp2(byte - 127.0)
    codes = (blocks / scale).astype(np.float32).astype(dtype).astype(np.float64)
    return np.moveaxis((codes * scale).reshape(v.shape), -1, axis)


WIDE = False


def mx_kscale(k):
    if not WIDE:
        return np.ones(k)
    levels = np.array([10, -10, 5, -5, 0])
    a = np.random.permutation(np.resize(levels, k // 512 * 4)).reshape(k // 512, 4)
    idx = np.arange(k)
    return np.exp2(a[idx // 512, idx % 128 // 32])


BF16 = ml_dtypes.bfloat16


def bf(x):
    return np.asarray(x, np.float32).astype(BF16)


def f64(x):
    return np.asarray(x).astype(np.float64)


B, S, D, H = 2, 512, 1024, 8
DH = D // H


def softmax(v, axis):
    e = np.exp(v - v.max(axis, keepdims=True))
    return e / e.sum(axis, keepdims=True)


def setup_inputs():
    s = mx_kscale(D)
    return {"x_k": bf(np.random.standard_normal((B, S, D)) * s),
            "W_K": bf(np.random.standard_normal((H, D, DH)) * 1.5 * DH ** 0.25 / np.sqrt(D) / s[:, None]),
            "v_heads": bf(np.random.standard_normal((B, H, S, DH)) * 2.0)}


def reference(x_k, W_K, v_heads):
    k = mxq(f64(x_k), 2, "e4m3")[:, None] @ mxq(f64(W_K), 1, "e4m3")[None]
    kt = softmax(np.swapaxes(k, -1, -2) / DH ** 0.25, -2)
    return mxq(kt, 3, "e4m3") @ mxq(f64(v_heads), 2, "e4m3")

@@ -1,0 +1,229 @@
+from contextlib import ExitStack
+
+import concourse.mybir as mybir
+from concourse.masks import make_identity
+
+F32 = mybir.dt.float32
+BF16 = mybir.dt.bfloat16
+U32 = mybir.dt.uint32
+U8 = mybir.dt.uint8
+FP8X4 = mybir.dt.float8_e4m3fn_x4
+ACT = mybir.ActivationFunctionType
+ALU = mybir.AluOpType
+AXIS = mybir.AxisListType
+
+B, S, D, H, DH = 2, 512, 1024, 8, 128
+P = 128
+PACK = 4
+K_PASS = P * PACK
+G = D // K_PASS
+TOKEN_TILES = B * S // P
+BANKS = B * H
+GROUP = 4
+SOFTMAX_SCALE = DH ** -0.25
+
+FLOPS = 2 * B * H * S * D * DH + 2 * B * H * S * DH * DH
+
+
+def tile_mhla2_pa_kernel(tc, x_k, W_K, v_heads, out):
+    nc = tc.nc
+    with ExitStack() as ctx:
+        keep = ctx.enter_context(tc.tile_pool(name="keep", bufs=1))
+        ring = ctx.enter_context(tc.tile_pool(name="ring", bufs=4))
+        psum_x = ctx.enter_context(tc.psum_pool(name="psum_x", bufs=2))
+        psum_k = ctx.enter_context(tc.psum_pool(name="psum_k", bufs=4))
+        psum_o = ctx.enter_context(tc.psum_pool(name="psum_o", bufs=2))
+
+        x_raw = keep.tile([P, TOKEN_TILES, D], BF16)
+        x_grouped = keep.tile([P, TOKEN_TILES, G, P * PACK], BF16, align_bytes=64)
+        x_codes = keep.tile([P, TOKEN_TILES, G, P], U32, align_bytes=64)
+        x_scales = keep.tile([P, TOKEN_TILES, G, P], U8, align_bytes=64)
+        w_raw = keep.tile([P, H * G, PACK, DH], BF16)
+        w_grouped = keep.tile([P, H * G, DH, PACK], BF16, align_bytes=64)
+        w_codes = keep.tile([P, H * G, DH], U32, align_bytes=64)
+        w_scales = keep.tile([P, H * G, DH], U8, align_bytes=64)
+        v_raw = keep.tile([P, BANKS, PACK, DH], BF16)
+        v_grouped = keep.tile([P, BANKS, DH, PACK], BF16, align_bytes=64)
+        v_codes = keep.tile([P, BANKS, DH], U32, align_bytes=64)
+        v_scales = keep.tile([P, BANKS, DH], U8, align_bytes=64)
+        p_codes = keep.tile([P, BANKS, DH], U32, align_bytes=64)
+        p_scales = keep.tile([P, BANKS, DH], U8, align_bytes=64)
+
+        def load_weights(h0, heads):
+            nc.sync.dma_start(
+                out=w_raw[:, h0 * G : (h0 + heads) * G],
+                in_=W_K[h0 : h0 + heads].rearrange("h (g p j) d -> p (h g) j d", g=G, j=PACK),
+            )
+
+        def load_tokens(b, t):
+            nc.sync.dma_start(
+                out=x_raw[:, PACK * b + t, :],
+                in_=x_k[b].rearrange("(p t) f -> p t f", t=PACK)[:, t, :],
+            )
+
+        def load_values(b):
+            nc.sync.dma_start(
+                out=v_raw[:, H * b : H * (b + 1)],
+                in_=v_heads[b].rearrange("h (p t) e -> p h t e", t=PACK),
+            )
+
+        load_weights(0, 2)
+        for t in range(PACK):
+            load_tokens(0, t)
+        load_weights(2, 2)
+        load_weights(4, 2)
+        load_weights(6, 2)
+        load_values(0)
+        for t in range(PACK):
+            load_tokens(1, t)
+        load_values(1)
+
+        identity = keep.tile([P, P], F32)
+        make_identity(nc, identity[:])
+
+        warm = keep.tile([P, 1], F32)
+        nc.vector.memset(warm[:], 0.0)
+        nc.scalar.activation(out=warm[:], in_=warm[:], func=ACT.Exp)
+
+        def regroup(engine_copy, grouped, raw):
+            engine_copy(
+                out=grouped.rearrange("p s (c i) j -> p s c j i", i=4),
+                in_=raw.rearrange("p s j (c i) -> p s c j i", i=4),
+            )
+
+        def transpose_tokens(tt):
+            words = x_raw[:, tt, :].bitcast(F32).rearrange("p (g q u) -> p g u q", g=G, u=2)
+            flipped = psum_x.tile([P, G, 2, P], F32)
+            for g in range(G):
+                for u in range(2):
+                    nc.tensor.transpose(flipped[:, g, u, :], words[:, g, u, :], identity[:])
+            nc.scalar.copy(
+                out=x_grouped[:, tt].bitcast(F32).rearrange("p g (n u) -> p g n u", u=2),
+                in_=flipped[:].rearrange("p g u n -> p g n u"),
+            )
+
+        def quantise_tokens(tt):
+            nc.vector.quantize_mx(
+                out=x_codes[:, tt].rearrange("p g n -> p (g n)").bitcast(FP8X4),
+                scales=x_scales[:, tt].rearrange("p g n -> p (g n)"),
+                in_=x_grouped[:, tt].rearrange("p g c -> p (g c)"),
+            )
+
+        def regroup_weights(h):
+            slabs = slice(h * G, (h + 1) * G)
+            if h % 2 == 0:
+                regroup(nc.vector.tensor_copy, w_grouped[:, slabs], w_raw[:, slabs])
+            else:
+                for c in range(h * G, (h + 1) * G):
+                    nc.scalar.copy(
+                        out=w_grouped[:, c].rearrange("p (c i) j -> p c j i", i=4),
+                        in_=w_raw[:, c].rearrange("p j (c i) -> p c j i", i=4),
+                    )
+
+        def quantise_weights(h):
+            slabs = slice(h * G, (h + 1) * G)
+            nc.vector.quantize_mx(
+                out=w_codes[:, slabs].rearrange("p s d -> p (s d)").bitcast(FP8X4),
+                scales=w_scales[:, slabs].rearrange("p s d -> p (s d)"),
+                in_=w_grouped[:, slabs].rearrange("p s d j -> p (s d j)"),
+            )
+
+        def regroup_values(i):
+            copy = nc.vector.tensor_copy if i % 2 == 0 else nc.scalar.copy
+            copy(
+                out=v_grouped[:, i].rearrange("p (c i) j -> p c j i", i=4),
+                in_=v_raw[:, i].rearrange("p j (c i) -> p c j i", i=4),
+            )
+
+        def quantise_values(i0):
+            banks = slice(i0, i0 + GROUP)
+            nc.vector.quantize_mx(
+                out=v_codes[:, banks].rearrange("p s d -> p (s d)").bitcast(FP8X4),
+                scales=v_scales[:, banks].rearrange("p s d -> p (s d)"),
+                in_=v_grouped[:, banks].rearrange("p s d j -> p (s d j)"),
+            )
+
+        def softmax_bank(i):
+            b, h = divmod(i, H)
+            k_bank = psum_k.tile([P, PACK, DH], F32)
+            for t in range(PACK):
+                for g in range(G):
+                    nc.tensor.matmul_mx(
+                        out=k_bank[:, t, :],
+                        lhsT=x_codes[:, PACK * b + t, g, :].bitcast(FP8X4),
+                        lhsT_scale=x_scales[:, PACK * b + t, g, :],
+                        rhs=w_codes[:, h * G + g, :].bitcast(FP8X4),
+                        rhs_scale=w_scales[:, h * G + g, :],
+                        start=(g == 0),
+                        stop=(g == G - 1),
+                    )
+            row_max = ring.tile([P, PACK], F32)
+            nc.vector.tensor_reduce(out=row_max[:], in_=k_bank[:], axis=AXIS.X, op=ALU.max)
+            shift = ring.tile([P, PACK], F32)
+            nc.scalar.mul(out=shift[:], in_=row_max[:], mul=-SOFTMAX_SCALE)
+            e = ring.tile([P, PACK, DH], F32)
+            row_sum = ring.tile([P, PACK], F32)
+            for t in range(PACK):
+                nc.scalar.activation(
+                    out=e[:, t, :],
+                    in_=k_bank[:, t, :],
+                    func=ACT.Exp,
+                    bias=shift[:, t : t + 1],
+                    scale=SOFTMAX_SCALE,
+                    accum_out=row_sum[:, t : t + 1],
+                )
+            inv_sum = ring.tile([P, PACK], F32)
+            nc.vector.reciprocal(out=inv_sum[:], in_=row_sum[:])
+            p_grouped = ring.tile([P, DH, PACK], BF16, align_bytes=64)
+            nc.vector.tensor_tensor(
+                out=p_grouped[:],
+                in0=e[:].rearrange("p t d -> p d t"),
+                in1=inv_sum[:].unsqueeze(1).to_broadcast([P, DH, PACK]),
+                op=ALU.mult,
+            )
+            nc.vector.quantize_mx(
+                out=p_codes[:, i, :].bitcast(FP8X4),
+                scales=p_scales[:, i, :],
+                in_=p_grouped[:].rearrange("p d t -> p (d t)"),
+            )
+
+        def summarise_group(i0):
+            b, h0 = divmod(i0, H)
+            o_bank = psum_o.tile([P, GROUP, DH], F32)
+            for n in range(GROUP):
+                nc.tensor.matmul_mx(
+                    out=o_bank[:, n, :],
+                    lhsT=p_codes[:, i0 + n, :].bitcast(FP8X4),
+                    lhsT_scale=p_scales[:, i0 + n, :],
+                    rhs=v_codes[:, i0 + n, :].bitcast(FP8X4),
+                    rhs_scale=v_scales[:, i0 + n, :],
+                    start=True,
+                    stop=True,
+                )
+            o_sb = ring.tile([P, GROUP, DH], F32)
+            nc.scalar.copy(out=o_sb[:], in_=o_bank[:])
+            nc.sync.dma_start(
+                out=out[b, h0 : h0 + GROUP].rearrange("h d e -> d h e"), in_=o_sb[:]
+            )
+
+        for h in range(H):
+            regroup_weights(h)
+        for t in range(PACK):
+            transpose_tokens(t)
+        for t in range(PACK):
+            quantise_tokens(t)
+        for h in range(H):
+            quantise_weights(h)
+        for b in range(B):
+            if b == 1:
+                for t in range(PACK):
+                    transpose_tokens(PACK + t)
+                for t in range(PACK):
+                    quantise_tokens(PACK + t)
+            for i in range(H * b, H * (b + 1)):
+                regroup_values(i)
+            for i0 in range(H * b, H * (b + 1), GROUP):
+                quantise_values(i0)
+                for i in range(i0, i0 + GROUP):
+                    softmax_bank(i)
+                summarise_group(i0)

@@ -19,7 +19,7 @@ K_PASS = P * PACK
 G = D // K_PASS
 TOKEN_TILES = B * S // P
 BANKS = B * H
-GROUP = 4
+PAIR = 2
 SOFTMAX_SCALE = DH ** -0.25
 
 FLOPS = 2 * B * H * S * D * DH + 2 * B * H * S * DH * DH
@@ -29,7 +29,7 @@ def tile_mhla2_pa_kernel(tc, x_k, W_K, v_heads, out):
     nc = tc.nc
     with ExitStack() as ctx:
         keep = ctx.enter_context(tc.tile_pool(name="keep", bufs=1))
-        ring = ctx.enter_context(tc.tile_pool(name="ring", bufs=4))
+        ring = ctx.enter_context(tc.tile_pool(name="ring", bufs=3))
         psum_x = ctx.enter_context(tc.psum_pool(name="psum_x", bufs=2))
         psum_k = ctx.enter_context(tc.psum_pool(name="psum_k", bufs=4))
         psum_o = ctx.enter_context(tc.psum_pool(name="psum_o", bufs=2))
@@ -49,10 +49,10 @@ def tile_mhla2_pa_kernel(tc, x_k, W_K, v_heads, out):
         p_codes = keep.tile([P, BANKS, DH], U32, align_bytes=64)
         p_scales = keep.tile([P, BANKS, DH], U8, align_bytes=64)
 
-        def load_weights(h0, heads):
+        def load_weights(h0):
             nc.sync.dma_start(
-                out=w_raw[:, h0 * G : (h0 + heads) * G],
-                in_=W_K[h0 : h0 + heads].rearrange("h (g p j) d -> p (h g) j d", g=G, j=PACK),
+                out=w_raw[:, h0 * G : (h0 + PAIR) * G],
+                in_=W_K[h0 : h0 + PAIR].rearrange("h (g p j) d -> p (h g) j d", g=G, j=PACK),
             )
 
         def load_tokens(b, t):
@@ -67,12 +67,11 @@ def tile_mhla2_pa_kernel(tc, x_k, W_K, v_heads, out):
                 in_=v_heads[b].rearrange("h (p t) e -> p h t e", t=PACK),
             )
 
-        load_weights(0, 2)
+        load_weights(0)
         for t in range(PACK):
             load_tokens(0, t)
-        load_weights(2, 2)
-        load_weights(4, 2)
-        load_weights(6, 2)
+        for h0 in range(PAIR, H, PAIR):
+            load_weights(h0)
         load_values(0)
         for t in range(PACK):
             load_tokens(1, t)
@@ -85,10 +84,11 @@ def tile_mhla2_pa_kernel(tc, x_k, W_K, v_heads, out):
         nc.vector.memset(warm[:], 0.0)
         nc.scalar.activation(out=warm[:], in_=warm[:], func=ACT.Exp)
 
-        def regroup(engine_copy, grouped, raw):
-            engine_copy(
-                out=grouped.rearrange("p s (c i) j -> p s c j i", i=4),
-                in_=raw.rearrange("p s j (c i) -> p s c j i", i=4),
+        def quantise(codes, scales, grouped):
+            nc.vector.quantize_mx(
+                out=codes.rearrange("p s n -> p (s n)").bitcast(FP8X4),
+                scales=scales.rearrange("p s n -> p (s n)"),
+                in_=grouped.rearrange("p s n j -> p (s n j)"),
             )
 
         def transpose_tokens(tt):
@@ -97,100 +97,86 @@ def tile_mhla2_pa_kernel(tc, x_k, W_K, v_heads, out):
             for g in range(G):
                 for u in range(2):
                     nc.tensor.transpose(flipped[:, g, u, :], words[:, g, u, :], identity[:])
-            nc.scalar.copy(
+            nc.any.tensor_copy(
                 out=x_grouped[:, tt].bitcast(F32).rearrange("p g (n u) -> p g n u", u=2),
                 in_=flipped[:].rearrange("p g u n -> p g n u"),
             )
 
-        def quantise_tokens(tt):
+        def quantise_tokens(tt, tiles):
             nc.vector.quantize_mx(
-                out=x_codes[:, tt].rearrange("p g n -> p (g n)").bitcast(FP8X4),
-                scales=x_scales[:, tt].rearrange("p g n -> p (g n)"),
-                in_=x_grouped[:, tt].rearrange("p g c -> p (g c)"),
+                out=x_codes[:, tt : tt + tiles].rearrange("p s g n -> p (s g n)").bitcast(FP8X4),
+                scales=x_scales[:, tt : tt + tiles].rearrange("p s g n -> p (s g n)"),
+                in_=x_grouped[:, tt : tt + tiles].rearrange("p s g c -> p (s g c)"),
             )
 
-        def regroup_weights(h):
-            slabs = slice(h * G, (h + 1) * G)
-            if h % 2 == 0:
-                regroup(nc.vector.tensor_copy, w_grouped[:, slabs], w_raw[:, slabs])
-            else:
-                for c in range(h * G, (h + 1) * G):
-                    nc.scalar.copy(
-                        out=w_grouped[:, c].rearrange("p (c i) j -> p c j i", i=4),
-                        in_=w_raw[:, c].rearrange("p j (c i) -> p c j i", i=4),
-                    )
-
-        def quantise_weights(h):
-            slabs = slice(h * G, (h + 1) * G)
-            nc.vector.quantize_mx(
-                out=w_codes[:, slabs].rearrange("p s d -> p (s d)").bitcast(FP8X4),
-                scales=w_scales[:, slabs].rearrange("p s d -> p (s d)"),
-                in_=w_grouped[:, slabs].rearrange("p s d j -> p (s d j)"),
-            )
-
-        def regroup_values(i):
-            copy = nc.vector.tensor_copy if i % 2 == 0 else nc.scalar.copy
-            copy(
-                out=v_grouped[:, i].rearrange("p (c i) j -> p c j i", i=4),
-                in_=v_raw[:, i].rearrange("p j (c i) -> p c j i", i=4),
-            )
-
-        def quantise_values(i0):
-            banks = slice(i0, i0 + GROUP)
-            nc.vector.quantize_mx(
-                out=v_codes[:, banks].rearrange("p s d -> p (s d)").bitcast(FP8X4),
-                scales=v_scales[:, banks].rearrange("p s d -> p (s d)"),
-                in_=v_grouped[:, banks].rearrange("p s d j -> p (s d j)"),
-            )
-
-        def softmax_bank(i):
-            b, h = divmod(i, H)
-            k_bank = psum_k.tile([P, PACK, DH], F32)
-            for t in range(PACK):
-                for g in range(G):
-                    nc.tensor.matmul_mx(
-                        out=k_bank[:, t, :],
-                        lhsT=x_codes[:, PACK * b + t, g, :].bitcast(FP8X4),
-                        lhsT_scale=x_scales[:, PACK * b + t, g, :],
-                        rhs=w_codes[:, h * G + g, :].bitcast(FP8X4),
-                        rhs_scale=w_scales[:, h * G + g, :],
-                        start=(g == 0),
-                        stop=(g == G - 1),
-                    )
-            row_max = ring.tile([P, PACK], F32)
-            nc.vector.tensor_reduce(out=row_max[:], in_=k_bank[:], axis=AXIS.X, op=ALU.max)
-            shift = ring.tile([P, PACK], F32)
-            nc.scalar.mul(out=shift[:], in_=row_max[:], mul=-SOFTMAX_SCALE)
-            e = ring.tile([P, PACK, DH], F32)
-            row_sum = ring.tile([P, PACK], F32)
-            for t in range(PACK):
-                nc.scalar.activation(
-                    out=e[:, t, :],
-                    in_=k_bank[:, t, :],
-                    func=ACT.Exp,
-                    bias=shift[:, t : t + 1],
-                    scale=SOFTMAX_SCALE,
-                    accum_out=row_sum[:, t : t + 1],
+        def prepare_weights(h0):
+            for c in range(h0 * G, (h0 + PAIR) * G):
+                nc.any.tensor_copy(
+                    out=w_grouped[:, c].rearrange("p (c i) j -> p c j i", i=4),
+                    in_=w_raw[:, c].rearrange("p j (c i) -> p c j i", i=4),
                 )
-            inv_sum = ring.tile([P, PACK], F32)
+
+        def quantise_weights(h0):
+            slabs = slice(h0 * G, (h0 + PAIR) * G)
+            quantise(w_codes[:, slabs], w_scales[:, slabs], w_grouped[:, slabs])
+
+        def prepare_values(i0):
+            for i in range(i0, i0 + PAIR):
+                nc.any.tensor_copy(
+                    out=v_grouped[:, i].rearrange("p (c i) j -> p c j i", i=4),
+                    in_=v_raw[:, i].rearrange("p j (c i) -> p c j i", i=4),
+                )
+
+        def quantise_values(i0, banks):
+            span = slice(i0, i0 + banks)
+            quantise(v_codes[:, span], v_scales[:, span], v_grouped[:, span])
+
+        def pair_of_heads(i0):
+            b, h0 = divmod(i0, H)
+            row_max = ring.tile([P, PAIR, PACK], F32)
+            k_banks = []
+            for n in range(PAIR):
+                k_bank = psum_k.tile([P, PACK, DH], F32)
+                k_banks.append(k_bank)
+                for t in range(PACK):
+                    for g in range(G):
+                        nc.tensor.matmul_mx(
+                            out=k_bank[:, t, :],
+                            lhsT=x_codes[:, PACK * b + t, g, :].bitcast(FP8X4),
+                            lhsT_scale=x_scales[:, PACK * b + t, g, :],
+                            rhs=w_codes[:, (h0 + n) * G + g, :].bitcast(FP8X4),
+                            rhs_scale=w_scales[:, (h0 + n) * G + g, :],
+                            start=(g == 0),
+                            stop=(g == G - 1),
+                        )
+                nc.vector.tensor_reduce(out=row_max[:, n, :], in_=k_bank[:], axis=AXIS.X, op=ALU.max)
+            shift = ring.tile([P, PAIR, PACK], F32)
+            nc.scalar.mul(out=shift[:], in_=row_max[:], mul=-SOFTMAX_SCALE)
+            e = ring.tile([P, PAIR, PACK, DH], F32)
+            row_sum = ring.tile([P, PAIR, PACK], F32)
+            for n in range(PAIR):
+                for t in range(PACK):
+                    nc.scalar.activation(
+                        out=e[:, n, t, :],
+                        in_=k_banks[n][:, t, :],
+                        func=ACT.Exp,
+                        bias=shift[:, n, t : t + 1],
+                        scale=SOFTMAX_SCALE,
+                        accum_out=row_sum[:, n, t : t + 1],
+                    )
+            inv_sum = ring.tile([P, PAIR, PACK], F32)
             nc.vector.reciprocal(out=inv_sum[:], in_=row_sum[:])
-            p_grouped = ring.tile([P, DH, PACK], BF16, align_bytes=64)
+            p_grouped = ring.tile([P, PAIR, DH, PACK], BF16, align_bytes=64)
             nc.vector.tensor_tensor(
                 out=p_grouped[:],
-                in0=e[:].rearrange("p t d -> p d t"),
-                in1=inv_sum[:].unsqueeze(1).to_broadcast([P, DH, PACK]),
+                in0=e[:].rearrange("p n t d -> p n d t"),
+                in1=inv_sum[:].unsqueeze(2).to_broadcast([P, PAIR, DH, PACK]),
                 op=ALU.mult,
             )
-            nc.vector.quantize_mx(
-                out=p_codes[:, i, :].bitcast(FP8X4),
-                scales=p_scales[:, i, :],
-                in_=p_grouped[:].rearrange("p d t -> p (d t)"),
-            )
-
-        def summarise_group(i0):
-            b, h0 = divmod(i0, H)
-            o_bank = psum_o.tile([P, GROUP, DH], F32)
-            for n in range(GROUP):
+            span = slice(i0, i0 + PAIR)
+            quantise(p_codes[:, span], p_scales[:, span], p_grouped[:])
+            o_bank = psum_o.tile([P, PAIR, DH], F32)
+            for n in range(PAIR):
                 nc.tensor.matmul_mx(
                     out=o_bank[:, n, :],
                     lhsT=p_codes[:, i0 + n, :].bitcast(FP8X4),
@@ -200,30 +186,29 @@ def tile_mhla2_pa_kernel(tc, x_k, W_K, v_heads, out):
                     start=True,
                     stop=True,
                 )
-            o_sb = ring.tile([P, GROUP, DH], F32)
-            nc.scalar.copy(out=o_sb[:], in_=o_bank[:])
+            o_sb = ring.tile([P, PAIR, DH], F32)
+            nc.any.tensor_copy(out=o_sb[:], in_=o_bank[:])
             nc.sync.dma_start(
-                out=out[b, h0 : h0 + GROUP].rearrange("h d e -> d h e"), in_=o_sb[:]
+                out=out[b, h0 : h0 + PAIR].rearrange("h d e -> d h e"), in_=o_sb[:]
             )
 
-        for h in range(H):
-            regroup_weights(h)
+        prepare_weights(0)
         for t in range(PACK):
             transpose_tokens(t)
+        quantise_weights(0)
         for t in range(PACK):
-            quantise_tokens(t)
-        for h in range(H):
-            quantise_weights(h)
+            quantise_tokens(t, 1)
+        for h0 in range(PAIR, H, PAIR):
+            prepare_weights(h0)
+            quantise_weights(h0)
         for b in range(B):
             if b == 1:
                 for t in range(PACK):
                     transpose_tokens(PACK + t)
-                for t in range(PACK):
-                    quantise_tokens(PACK + t)
-            for i in range(H * b, H * (b + 1)):
-                regroup_values(i)
-            for i0 in range(H * b, H * (b + 1), GROUP):
-                quantise_values(i0)
-                for i in range(i0, i0 + GROUP):
-                    softmax_bank(i)
-                summarise_group(i0)
+                quantise_tokens(PACK, PACK)
+            for i0 in range(H * b, H * (b + 1), 2 * PAIR):
+                prepare_values(i0)
+                prepare_values(i0 + PAIR)
+                quantise_values(i0, 2 * PAIR)
+                pair_of_heads(i0)
+                pair_of_heads(i0 + PAIR)

@@ -29,10 +29,11 @@ def tile_mhla2_pa_kernel(tc, x_k, W_K, v_heads, out):
     nc = tc.nc
     with ExitStack() as ctx:
         keep = ctx.enter_context(tc.tile_pool(name="keep", bufs=1))
-        ring = ctx.enter_context(tc.tile_pool(name="ring", bufs=3))
+        ring = ctx.enter_context(tc.tile_pool(name="ring", bufs=4))
         psum_x = ctx.enter_context(tc.psum_pool(name="psum_x", bufs=2))
         psum_k = ctx.enter_context(tc.psum_pool(name="psum_k", bufs=4))
         psum_o = ctx.enter_context(tc.psum_pool(name="psum_o", bufs=2))
+        ctx.enter_context(tc.manual_schedule())
 
         x_raw = keep.tile([P, TOKEN_TILES, D], BF16)
         x_grouped = keep.tile([P, TOKEN_TILES, G, P * PACK], BF16, align_bytes=64)
@@ -49,10 +50,10 @@ def tile_mhla2_pa_kernel(tc, x_k, W_K, v_heads, out):
         p_codes = keep.tile([P, BANKS, DH], U32, align_bytes=64)
         p_scales = keep.tile([P, BANKS, DH], U8, align_bytes=64)
 
-        def load_weights(h0):
+        def load_weights(h0, heads):
             nc.sync.dma_start(
-                out=w_raw[:, h0 * G : (h0 + PAIR) * G],
-                in_=W_K[h0 : h0 + PAIR].rearrange("h (g p j) d -> p (h g) j d", g=G, j=PACK),
+                out=w_raw[:, h0 * G : (h0 + heads) * G],
+                in_=W_K[h0 : h0 + heads].rearrange("h (g p j) d -> p (h g) j d", g=G, j=PACK),
             )
 
         def load_tokens(b, t):
@@ -67,11 +68,12 @@ def tile_mhla2_pa_kernel(tc, x_k, W_K, v_heads, out):
                 in_=v_heads[b].rearrange("h (p t) e -> p h t e", t=PACK),
             )
 
-        load_weights(0)
+        load_weights(0, 2)
         for t in range(PACK):
             load_tokens(0, t)
-        for h0 in range(PAIR, H, PAIR):
-            load_weights(h0)
+        load_weights(2, 2)
+        load_weights(4, 2)
+        load_weights(6, 2)
         load_values(0)
         for t in range(PACK):
             load_tokens(1, t)
@@ -84,131 +86,177 @@ def tile_mhla2_pa_kernel(tc, x_k, W_K, v_heads, out):
         nc.vector.memset(warm[:], 0.0)
         nc.scalar.activation(out=warm[:], in_=warm[:], func=ACT.Exp)
 
-        def quantise(codes, scales, grouped):
-            nc.vector.quantize_mx(
-                out=codes.rearrange("p s n -> p (s n)").bitcast(FP8X4),
-                scales=scales.rearrange("p s n -> p (s n)"),
-                in_=grouped.rearrange("p s n j -> p (s n j)"),
-            )
-
         def transpose_tokens(tt):
             words = x_raw[:, tt, :].bitcast(F32).rearrange("p (g q u) -> p g u q", g=G, u=2)
             flipped = psum_x.tile([P, G, 2, P], F32)
             for g in range(G):
                 for u in range(2):
                     nc.tensor.transpose(flipped[:, g, u, :], words[:, g, u, :], identity[:])
-            nc.any.tensor_copy(
+            nc.scalar.copy(
                 out=x_grouped[:, tt].bitcast(F32).rearrange("p g (n u) -> p g n u", u=2),
                 in_=flipped[:].rearrange("p g u n -> p g n u"),
             )
 
-        def quantise_tokens(tt, tiles):
+        def quantise_tokens(tt):
             nc.vector.quantize_mx(
-                out=x_codes[:, tt : tt + tiles].rearrange("p s g n -> p (s g n)").bitcast(FP8X4),
-                scales=x_scales[:, tt : tt + tiles].rearrange("p s g n -> p (s g n)"),
-                in_=x_grouped[:, tt : tt + tiles].rearrange("p s g c -> p (s g c)"),
+                out=x_codes[:, tt].rearrange("p g n -> p (g n)").bitcast(FP8X4),
+                scales=x_scales[:, tt].rearrange("p g n -> p (g n)"),
+                in_=x_grouped[:, tt].rearrange("p g c -> p (g c)"),
             )
 
-        def prepare_weights(h0):
-            for c in range(h0 * G, (h0 + PAIR) * G):
-                nc.any.tensor_copy(
-                    out=w_grouped[:, c].rearrange("p (c i) j -> p c j i", i=4),
-                    in_=w_raw[:, c].rearrange("p j (c i) -> p c j i", i=4),
+        def regroup_weights(h):
+            slabs = slice(h * G, (h + 1) * G)
+            if h % 2 == 0:
+                nc.vector.tensor_copy(
+                    out=w_grouped[:, slabs].rearrange("p s (c i) j -> p s c j i", i=4),
+                    in_=w_raw[:, slabs].rearrange("p s j (c i) -> p s c j i", i=4),
                 )
-
-        def quantise_weights(h0):
-            slabs = slice(h0 * G, (h0 + PAIR) * G)
-            quantise(w_codes[:, slabs], w_scales[:, slabs], w_grouped[:, slabs])
-
-        def prepare_values(i0):
-            for i in range(i0, i0 + PAIR):
-                nc.any.tensor_copy(
-                    out=v_grouped[:, i].rearrange("p (c i) j -> p c j i", i=4),
-                    in_=v_raw[:, i].rearrange("p j (c i) -> p c j i", i=4),
-                )
-
-        def quantise_values(i0, banks):
-            span = slice(i0, i0 + banks)
-            quantise(v_codes[:, span], v_scales[:, span], v_grouped[:, span])
-
-        def pair_of_heads(i0):
-            b, h0 = divmod(i0, H)
-            row_max = ring.tile([P, PAIR, PACK], F32)
-            k_banks = []
-            for n in range(PAIR):
-                k_bank = psum_k.tile([P, PACK, DH], F32)
-                k_banks.append(k_bank)
-                for t in range(PACK):
-                    for g in range(G):
-                        nc.tensor.matmul_mx(
-                            out=k_bank[:, t, :],
-                            lhsT=x_codes[:, PACK * b + t, g, :].bitcast(FP8X4),
-                            lhsT_scale=x_scales[:, PACK * b + t, g, :],
-                            rhs=w_codes[:, (h0 + n) * G + g, :].bitcast(FP8X4),
-                            rhs_scale=w_scales[:, (h0 + n) * G + g, :],
-                            start=(g == 0),
-                            stop=(g == G - 1),
-                        )
-                nc.vector.tensor_reduce(out=row_max[:, n, :], in_=k_bank[:], axis=AXIS.X, op=ALU.max)
-            shift = ring.tile([P, PAIR, PACK], F32)
-            nc.scalar.mul(out=shift[:], in_=row_max[:], mul=-SOFTMAX_SCALE)
-            e = ring.tile([P, PAIR, PACK, DH], F32)
-            row_sum = ring.tile([P, PAIR, PACK], F32)
-            for n in range(PAIR):
-                for t in range(PACK):
-                    nc.scalar.activation(
-                        out=e[:, n, t, :],
-                        in_=k_banks[n][:, t, :],
-                        func=ACT.Exp,
-                        bias=shift[:, n, t : t + 1],
-                        scale=SOFTMAX_SCALE,
-                        accum_out=row_sum[:, n, t : t + 1],
+            else:
+                for c in range(h * G, (h + 1) * G):
+                    nc.scalar.copy(
+                        out=w_grouped[:, c].rearrange("p (c i) j -> p c j i", i=4),
+                        in_=w_raw[:, c].rearrange("p j (c i) -> p c j i", i=4),
                     )
-            inv_sum = ring.tile([P, PAIR, PACK], F32)
-            nc.vector.reciprocal(out=inv_sum[:], in_=row_sum[:])
-            p_grouped = ring.tile([P, PAIR, DH, PACK], BF16, align_bytes=64)
+
+        def quantise_weights(h):
+            slabs = slice(h * G, (h + 1) * G)
+            nc.vector.quantize_mx(
+                out=w_codes[:, slabs].rearrange("p s d -> p (s d)").bitcast(FP8X4),
+                scales=w_scales[:, slabs].rearrange("p s d -> p (s d)"),
+                in_=w_grouped[:, slabs].rearrange("p s d j -> p (s d j)"),
+            )
+
+        def regroup_values(i):
+            copy = nc.vector.tensor_copy if i % 2 == 0 else nc.scalar.copy
+            copy(
+                out=v_grouped[:, i].rearrange("p (c i) j -> p c j i", i=4),
+                in_=v_raw[:, i].rearrange("p j (c i) -> p c j i", i=4),
+            )
+
+        def quantise_values(i0):
+            banks = slice(i0, i0 + PAIR)
+            nc.vector.quantize_mx(
+                out=v_codes[:, banks].rearrange("p s d -> p (s d)").bitcast(FP8X4),
+                scales=v_scales[:, banks].rearrange("p s d -> p (s d)"),
+                in_=v_grouped[:, banks].rearrange("p s d j -> p (s d j)"),
+            )
+
+        k_banks, shifts, exps, row_sums, inv_sums, p_groupeds, o_banks = {}, {}, {}, {}, {}, {}, {}
+
+        def project(i):
+            b, h = divmod(i, H)
+            k_banks[i] = psum_k.tile([P, PACK, DH], F32, name="k_bank")
+            for t in range(PACK):
+                for g in range(G):
+                    nc.tensor.matmul_mx(
+                        out=k_banks[i][:, t, :],
+                        lhsT=x_codes[:, PACK * b + t, g, :].bitcast(FP8X4),
+                        lhsT_scale=x_scales[:, PACK * b + t, g, :],
+                        rhs=w_codes[:, h * G + g, :].bitcast(FP8X4),
+                        rhs_scale=w_scales[:, h * G + g, :],
+                        start=(g == 0),
+                        stop=(g == G - 1),
+                    )
+
+        def exponentials(i):
+            row_max = ring.tile([P, PACK], F32)
+            nc.vector.tensor_reduce(out=row_max[:], in_=k_banks[i][:], axis=AXIS.X, op=ALU.max)
+            shift = ring.tile([P, PACK], F32)
+            nc.scalar.mul(out=shift[:], in_=row_max[:], mul=-SOFTMAX_SCALE)
+            exps[i] = ring.tile([P, PACK, DH], F32, name="e")
+            row_sums[i] = ring.tile([P, PACK], F32, name="row_sum")
+            for t in range(PACK):
+                nc.scalar.activation(
+                    out=exps[i][:, t, :],
+                    in_=k_banks[i][:, t, :],
+                    func=ACT.Exp,
+                    bias=shift[:, t : t + 1],
+                    scale=SOFTMAX_SCALE,
+                    accum_out=row_sums[i][:, t : t + 1],
+                )
+
+        def invert_sums(i):
+            inv_sums[i] = ring.tile([P, PACK], F32, name="inv_sum")
+            nc.vector.reciprocal(out=inv_sums[i][:], in_=row_sums[i][:])
+
+        def normalise(i):
+            p_groupeds[i] = ring.tile([P, DH, PACK], BF16, name="p_grouped", align_bytes=64)
             nc.vector.tensor_tensor(
-                out=p_grouped[:],
-                in0=e[:].rearrange("p n t d -> p n d t"),
-                in1=inv_sum[:].unsqueeze(2).to_broadcast([P, PAIR, DH, PACK]),
+                out=p_groupeds[i][:],
+                in0=exps[i][:].rearrange("p t d -> p d t"),
+                in1=inv_sums[i][:].unsqueeze(1).to_broadcast([P, DH, PACK]),
                 op=ALU.mult,
             )
-            span = slice(i0, i0 + PAIR)
-            quantise(p_codes[:, span], p_scales[:, span], p_grouped[:])
-            o_bank = psum_o.tile([P, PAIR, DH], F32)
-            for n in range(PAIR):
-                nc.tensor.matmul_mx(
-                    out=o_bank[:, n, :],
-                    lhsT=p_codes[:, i0 + n, :].bitcast(FP8X4),
-                    lhsT_scale=p_scales[:, i0 + n, :],
-                    rhs=v_codes[:, i0 + n, :].bitcast(FP8X4),
-                    rhs_scale=v_scales[:, i0 + n, :],
-                    start=True,
-                    stop=True,
-                )
+
+        def quantise_probabilities(i):
+            nc.vector.quantize_mx(
+                out=p_codes[:, i, :].bitcast(FP8X4),
+                scales=p_scales[:, i, :],
+                in_=p_groupeds[i][:].rearrange("p d t -> p (d t)"),
+            )
+
+        def summarise(i):
+            i0 = i - i % PAIR
+            if i == i0:
+                o_banks[i0] = psum_o.tile([P, PAIR, DH], F32, name="o_bank")
+            nc.tensor.matmul_mx(
+                out=o_banks[i0][:, i - i0, :],
+                lhsT=p_codes[:, i, :].bitcast(FP8X4),
+                lhsT_scale=p_scales[:, i, :],
+                rhs=v_codes[:, i, :].bitcast(FP8X4),
+                rhs_scale=v_scales[:, i, :],
+                start=True,
+                stop=True,
+            )
+
+        def store_pair(i0):
+            b, h0 = divmod(i0, H)
             o_sb = ring.tile([P, PAIR, DH], F32)
-            nc.any.tensor_copy(out=o_sb[:], in_=o_bank[:])
+            nc.scalar.copy(out=o_sb[:], in_=o_banks[i0][:])
             nc.sync.dma_start(
                 out=out[b, h0 : h0 + PAIR].rearrange("h d e -> d h e"), in_=o_sb[:]
             )
 
-        prepare_weights(0)
-        for t in range(PACK):
-            transpose_tokens(t)
+        regroup_weights(0)
+        regroup_weights(1)
         quantise_weights(0)
         for t in range(PACK):
-            quantise_tokens(t, 1)
-        for h0 in range(PAIR, H, PAIR):
-            prepare_weights(h0)
-            quantise_weights(h0)
-        for b in range(B):
-            if b == 1:
-                for t in range(PACK):
-                    transpose_tokens(PACK + t)
-                quantise_tokens(PACK, PACK)
-            for i0 in range(H * b, H * (b + 1), 2 * PAIR):
-                prepare_values(i0)
-                prepare_values(i0 + PAIR)
-                quantise_values(i0, 2 * PAIR)
-                pair_of_heads(i0)
-                pair_of_heads(i0 + PAIR)
+            transpose_tokens(t)
+        quantise_weights(1)
+        quantise_tokens(0)
+        quantise_tokens(1)
+        regroup_weights(2)
+        quantise_tokens(2)
+        quantise_tokens(3)
+        regroup_weights(3)
+        project(0)
+        quantise_weights(2)
+
+        for s in range(BANKS + 4):
+            if s < BANKS:
+                exponentials(s)
+            if s == 0:
+                quantise_weights(3)
+            if 4 <= s < 4 + PACK:
+                quantise_tokens(PACK + s - 4)
+            if s + 1 < BANKS:
+                project(s + 1)
+            if 3 <= s < 3 + PACK:
+                transpose_tokens(PACK + s - 3)
+            if 0 <= s - 2 < BANKS:
+                invert_sums(s - 2)
+            if s + 4 < H:
+                regroup_weights(s + 4)
+            if 0 <= s - 1 < BANKS:
+                regroup_values(s - 1)
+            if 0 <= s - 2 < BANKS and (s - 2) % PAIR == PAIR - 1:
+                quantise_values(s - 2 - (PAIR - 1))
+            if 0 <= s - 3 < BANKS:
+                quantise_probabilities(s - 3)
+                summarise(s - 3)
+            if 0 <= s - 2 < BANKS:
+                normalise(s - 2)
+            if 1 <= s and s + 3 < H:
+                quantise_weights(s + 3)
+            if 0 <= s - 3 < BANKS and (s - 3) % PAIR == PAIR - 1:
+                store_pair(s - 3 - (PAIR - 1))

@@ -62,22 +62,28 @@ def tile_mhla2_pa_kernel(tc, x_k, W_K, v_heads, out):
                 in_=x_k[b].rearrange("(p t) f -> p t f", t=PACK)[:, t, :],
             )
 
-        def load_values(b):
+        def load_values(b, h0, heads):
             nc.sync.dma_start(
-                out=v_raw[:, H * b : H * (b + 1)],
-                in_=v_heads[b].rearrange("h (p t) e -> p h t e", t=PACK),
+                out=v_raw[:, H * b + h0 : H * b + h0 + heads],
+                in_=v_heads[b, h0 : h0 + heads].rearrange("h (p t) e -> p h t e", t=PACK),
             )
 
-        load_weights(0, 2)
-        for t in range(PACK):
-            load_tokens(0, t)
-        load_weights(2, 2)
+        load_weights(0, 1)
+        load_weights(1, 1)
+        load_tokens(0, 0)
+        load_tokens(0, 1)
+        load_weights(2, 1)
+        load_tokens(0, 2)
+        load_tokens(0, 3)
+        load_weights(3, 1)
+        load_values(0, 0, 2)
         load_weights(4, 2)
+        load_values(0, 2, 2)
         load_weights(6, 2)
-        load_values(0)
         for t in range(PACK):
             load_tokens(1, t)
-        load_values(1)
+        load_values(0, 4, 4)
+        load_values(1, 0, 8)
 
         identity = keep.tile([P, P], F32)
         make_identity(nc, identity[:])
@@ -88,7 +94,7 @@ def tile_mhla2_pa_kernel(tc, x_k, W_K, v_heads, out):
 
         def transpose_tokens(tt):
             words = x_raw[:, tt, :].bitcast(F32).rearrange("p (g q u) -> p g u q", g=G, u=2)
-            flipped = psum_x.tile([P, G, 2, P], F32)
+            flipped = psum_x.tile([P, G, 2, P], F32, name="flipped")
             for g in range(G):
                 for u in range(2):
                     nc.tensor.transpose(flipped[:, g, u, :], words[:, g, u, :], identity[:])
@@ -104,37 +110,36 @@ def tile_mhla2_pa_kernel(tc, x_k, W_K, v_heads, out):
                 in_=x_grouped[:, tt].rearrange("p g c -> p (g c)"),
             )
 
-        def regroup_weights(h):
+        def regroup_weights_vector(h):
             slabs = slice(h * G, (h + 1) * G)
-            if h % 2 == 0:
-                nc.vector.tensor_copy(
-                    out=w_grouped[:, slabs].rearrange("p s (c i) j -> p s c j i", i=4),
-                    in_=w_raw[:, slabs].rearrange("p s j (c i) -> p s c j i", i=4),
-                )
-            else:
-                for c in range(h * G, (h + 1) * G):
-                    nc.scalar.copy(
-                        out=w_grouped[:, c].rearrange("p (c i) j -> p c j i", i=4),
-                        in_=w_raw[:, c].rearrange("p j (c i) -> p c j i", i=4),
-                    )
+            nc.vector.tensor_copy(
+                out=w_grouped[:, slabs].rearrange("p s (c i) j -> p s c j i", i=4),
+                in_=w_raw[:, slabs].rearrange("p s j (c i) -> p s c j i", i=4),
+            )
 
-        def quantise_weights(h):
-            slabs = slice(h * G, (h + 1) * G)
+        def regroup_weights_scalar(h):
+            for c in range(h * G, (h + 1) * G):
+                nc.scalar.copy(
+                    out=w_grouped[:, c].rearrange("p (c i) j -> p c j i", i=4),
+                    in_=w_raw[:, c].rearrange("p j (c i) -> p c j i", i=4),
+                )
+
+        def quantise_weights(h0, heads):
+            slabs = slice(h0 * G, (h0 + heads) * G)
             nc.vector.quantize_mx(
                 out=w_codes[:, slabs].rearrange("p s d -> p (s d)").bitcast(FP8X4),
                 scales=w_scales[:, slabs].rearrange("p s d -> p (s d)"),
                 in_=w_grouped[:, slabs].rearrange("p s d j -> p (s d j)"),
             )
 
-        def regroup_values(i):
-            copy = nc.vector.tensor_copy if i % 2 == 0 else nc.scalar.copy
+        def regroup_values(copy, i):
             copy(
                 out=v_grouped[:, i].rearrange("p (c i) j -> p c j i", i=4),
                 in_=v_raw[:, i].rearrange("p j (c i) -> p c j i", i=4),
             )
 
-        def quantise_values(i0):
-            banks = slice(i0, i0 + PAIR)
+        def quantise_values(i0, n):
+            banks = slice(i0, i0 + n)
             nc.vector.quantize_mx(
                 out=v_codes[:, banks].rearrange("p s d -> p (s d)").bitcast(FP8X4),
                 scales=v_scales[:, banks].rearrange("p s d -> p (s d)"),
@@ -158,105 +163,151 @@ def tile_mhla2_pa_kernel(tc, x_k, W_K, v_heads, out):
                         stop=(g == G - 1),
                     )
 
-        def exponentials(i):
-            row_max = ring.tile([P, PACK], F32)
+        def maxima(i):
+            row_max = ring.tile([P, PACK], F32, name="row_max")
             nc.vector.tensor_reduce(out=row_max[:], in_=k_banks[i][:], axis=AXIS.X, op=ALU.max)
-            shift = ring.tile([P, PACK], F32)
-            nc.scalar.mul(out=shift[:], in_=row_max[:], mul=-SOFTMAX_SCALE)
-            exps[i] = ring.tile([P, PACK, DH], F32, name="e")
-            row_sums[i] = ring.tile([P, PACK], F32, name="row_sum")
+            shifts[i] = row_max
+
+        def shift_scale(i):
+            shift = ring.tile([P, PACK], F32, name="shift")
+            nc.scalar.mul(out=shift[:], in_=shifts[i][:], mul=-SOFTMAX_SCALE)
+            shifts[i] = shift
+
+        def exponentials(i):
+            j, n = divmod(i, PAIR)
+            shift = shifts[i]
+            if n == 0:
+                exps[j] = ring.tile([P, PAIR, PACK, DH], F32, name="e")
+                row_sums[j] = ring.tile([P, PAIR, PACK], F32, name="row_sum")
             for t in range(PACK):
                 nc.scalar.activation(
-                    out=exps[i][:, t, :],
+                    out=exps[j][:, n, t, :],
                     in_=k_banks[i][:, t, :],
                     func=ACT.Exp,
                     bias=shift[:, t : t + 1],
                     scale=SOFTMAX_SCALE,
-                    accum_out=row_sums[i][:, t : t + 1],
+                    accum_out=row_sums[j][:, n, t : t + 1],
                 )
 
-        def invert_sums(i):
-            inv_sums[i] = ring.tile([P, PACK], F32, name="inv_sum")
-            nc.vector.reciprocal(out=inv_sums[i][:], in_=row_sums[i][:])
+        def invert_sums(i0, n):
+            j, n0 = divmod(i0, PAIR)
+            if n0 == 0:
+                inv_sums[j] = ring.tile([P, PAIR, PACK], F32, name="inv_sum")
+                p_groupeds[j] = ring.tile([P, PAIR, DH, PACK], BF16, name="p_grouped", align_bytes=64)
+            nc.vector.reciprocal(
+                out=inv_sums[j][:, n0 : n0 + n], in_=row_sums[j][:, n0 : n0 + n]
+            )
 
-        def normalise(i):
-            p_groupeds[i] = ring.tile([P, DH, PACK], BF16, name="p_grouped", align_bytes=64)
+        def normalise(i0, n):
+            j, n0 = divmod(i0, PAIR)
             nc.vector.tensor_tensor(
-                out=p_groupeds[i][:],
-                in0=exps[i][:].rearrange("p t d -> p d t"),
-                in1=inv_sums[i][:].unsqueeze(1).to_broadcast([P, DH, PACK]),
+                out=p_groupeds[j][:, n0 : n0 + n],
+                in0=exps[j][:, n0 : n0 + n].rearrange("p n t d -> p n d t"),
+                in1=inv_sums[j][:, n0 : n0 + n].unsqueeze(2).to_broadcast([P, n, DH, PACK]),
                 op=ALU.mult,
             )
 
-        def quantise_probabilities(i):
+        def quantise_probabilities(i0, n):
+            j, n0 = divmod(i0, PAIR)
+            banks = slice(i0, i0 + n)
             nc.vector.quantize_mx(
-                out=p_codes[:, i, :].bitcast(FP8X4),
-                scales=p_scales[:, i, :],
-                in_=p_groupeds[i][:].rearrange("p d t -> p (d t)"),
+                out=p_codes[:, banks].rearrange("p n d -> p (n d)").bitcast(FP8X4),
+                scales=p_scales[:, banks].rearrange("p n d -> p (n d)"),
+                in_=p_groupeds[j][:, n0 : n0 + n].rearrange("p n d t -> p (n d t)"),
             )
 
-        def summarise(i):
-            i0 = i - i % PAIR
-            if i == i0:
-                o_banks[i0] = psum_o.tile([P, PAIR, DH], F32, name="o_bank")
-            nc.tensor.matmul_mx(
-                out=o_banks[i0][:, i - i0, :],
-                lhsT=p_codes[:, i, :].bitcast(FP8X4),
-                lhsT_scale=p_scales[:, i, :],
-                rhs=v_codes[:, i, :].bitcast(FP8X4),
-                rhs_scale=v_scales[:, i, :],
-                start=True,
-                stop=True,
-            )
+        def summarise(i0, n):
+            j, n0 = divmod(i0, PAIR)
+            if n0 == 0:
+                o_banks[j] = psum_o.tile([P, PAIR, DH], F32, name="o_bank")
+            for i in range(i0, i0 + n):
+                nc.tensor.matmul_mx(
+                    out=o_banks[j][:, i % PAIR, :],
+                    lhsT=p_codes[:, i, :].bitcast(FP8X4),
+                    lhsT_scale=p_scales[:, i, :],
+                    rhs=v_codes[:, i, :].bitcast(FP8X4),
+                    rhs_scale=v_scales[:, i, :],
+                    start=True,
+                    stop=True,
+                )
 
-        def store_pair(i0):
+        def store(i0, n):
+            j, n0 = divmod(i0, PAIR)
             b, h0 = divmod(i0, H)
-            o_sb = ring.tile([P, PAIR, DH], F32)
-            nc.scalar.copy(out=o_sb[:], in_=o_banks[i0][:])
+            o_sb = ring.tile([P, PAIR, DH], F32, name="o_sb")
+            nc.scalar.copy(out=o_sb[:, :n], in_=o_banks[j][:, n0 : n0 + n])
             nc.sync.dma_start(
-                out=out[b, h0 : h0 + PAIR].rearrange("h d e -> d h e"), in_=o_sb[:]
+                out=out[b, h0 : h0 + n].rearrange("h d e -> d h e"), in_=o_sb[:, :n]
             )
 
-        regroup_weights(0)
-        regroup_weights(1)
-        quantise_weights(0)
+        regroup_weights_vector(0)
+        regroup_weights_scalar(1)
+        quantise_weights(0, 1)
         for t in range(PACK):
             transpose_tokens(t)
-        quantise_weights(1)
+        quantise_weights(1, 1)
         quantise_tokens(0)
+        regroup_weights_vector(2)
         quantise_tokens(1)
-        regroup_weights(2)
         quantise_tokens(2)
+        quantise_weights(2, 1)
         quantise_tokens(3)
-        regroup_weights(3)
         project(0)
-        quantise_weights(2)
-
-        for s in range(BANKS + 4):
-            if s < BANKS:
-                exponentials(s)
-            if s == 0:
-                quantise_weights(3)
-            if 4 <= s < 4 + PACK:
-                quantise_tokens(PACK + s - 4)
-            if s + 1 < BANKS:
-                project(s + 1)
-            if 3 <= s < 3 + PACK:
-                transpose_tokens(PACK + s - 3)
-            if 0 <= s - 2 < BANKS:
-                invert_sums(s - 2)
-            if s + 4 < H:
-                regroup_weights(s + 4)
-            if 0 <= s - 1 < BANKS:
-                regroup_values(s - 1)
-            if 0 <= s - 2 < BANKS and (s - 2) % PAIR == PAIR - 1:
-                quantise_values(s - 2 - (PAIR - 1))
-            if 0 <= s - 3 < BANKS:
-                quantise_probabilities(s - 3)
-                summarise(s - 3)
-            if 0 <= s - 2 < BANKS:
-                normalise(s - 2)
-            if 1 <= s and s + 3 < H:
-                quantise_weights(s + 3)
-            if 0 <= s - 3 < BANKS and (s - 3) % PAIR == PAIR - 1:
-                store_pair(s - 3 - (PAIR - 1))
+        regroup_weights_vector(3)
+        regroup_values(nc.scalar.copy, 0)
+        regroup_values(nc.scalar.copy, 1)
+        maxima(0)
+        shift_scale(0)
+        project(1)
+        maxima(1)
+        quantise_weights(3, 1)
+        LAST = BANKS - 1
+        for i in range(BANKS + 3):
+            j, n = divmod(i, PAIR)
+            if i < BANKS:
+                exponentials(i)
+            if n == 0 and 1 <= j < BANKS // PAIR:
+                invert_sums(i - PAIR, PAIR)
+            if i >= LAST:
+                if i <= LAST + 1:
+                    invert_sums(i - 1, 1)
+            if 1 <= i and i + 1 < BANKS:
+                maxima(i + 1)
+            if i + 1 < BANKS:
+                shift_scale(i + 1)
+            if n == 0 and 1 <= j < BANKS // PAIR:
+                normalise(i - PAIR, PAIR)
+            if LAST <= i <= LAST + 1:
+                normalise(i - 1, 1)
+            if 3 <= i < 7:
+                quantise_tokens(i + 1)
+            if i + 2 < BANKS:
+                project(i + 2)
+            if i in (0, 1):
+                regroup_weights_vector(4 + 2 * i)
+                regroup_weights_scalar(5 + 2 * i)
+            if i in (1, 3):
+                quantise_weights(i + 3, 2)
+            if 2 <= i < BANKS - 1:
+                if i in (9, 11, 13):
+                    regroup_values(nc.vector.tensor_copy, i)
+                else:
+                    regroup_values(nc.scalar.copy, i)
+                if i == BANKS - 2:
+                    regroup_values(nc.vector.tensor_copy, i + 1)
+            if 2 <= i < 6:
+                transpose_tokens(i + 2)
+            if n == 1 and 1 <= j <= BANKS // PAIR:
+                if j < BANKS // PAIR:
+                    quantise_values(PAIR * (j - 1), PAIR)
+                    quantise_probabilities(i - 1 - PAIR, PAIR)
+                    summarise(i - 1 - PAIR, PAIR)
+            if i == LAST:
+                quantise_values(BANKS - PAIR, PAIR)
+            if LAST <= i <= LAST + 1:
+                quantise_probabilities(i - 1, 1)
+                summarise(i - 1, 1)
+            if n == 0 and 2 <= j <= BANKS // PAIR:
+                store(i - 2 * PAIR, PAIR)
+            if LAST + 1 <= i <= LAST + 2:
+                store(i - 2, 1)

@@ -69,24 +69,26 @@ def tile_mhla2_pa_kernel(tc, x_k, W_K, v_heads, out):
             )
 
         load_weights(0, 1)
-        load_weights(1, 1)
         load_tokens(0, 0)
+        load_weights(1, 1)
         load_tokens(0, 1)
-        load_weights(2, 1)
         load_tokens(0, 2)
         load_tokens(0, 3)
+        load_weights(2, 1)
         load_weights(3, 1)
+        load_weights(4, 1)
         load_values(0, 0, 2)
-        load_weights(4, 2)
-        load_values(0, 2, 2)
+        load_weights(5, 1)
         load_weights(6, 2)
         for t in range(PACK):
             load_tokens(1, t)
-        load_values(0, 4, 4)
+        load_values(0, 2, 6)
         load_values(1, 0, 8)
 
         identity = keep.tile([P, P], F32)
         make_identity(nc, identity[:])
+        identity_bf16 = keep.tile([P, P], BF16)
+        make_identity(nc, identity_bf16[:])
 
         warm = keep.tile([P, 1], F32)
         nc.vector.memset(warm[:], 0.0)
@@ -132,6 +134,21 @@ def tile_mhla2_pa_kernel(tc, x_k, W_K, v_heads, out):
                 in_=w_grouped[:, slabs].rearrange("p s d j -> p (s d j)"),
             )
 
+        def flip_values(j):
+            flipped = psum_x.tile([P, PAIR, DH, PACK], BF16, name="flipped")
+            for n in range(PAIR):
+                nc.tensor.matmul(
+                    flipped[:, n],
+                    lhsT=identity_bf16[:],
+                    rhs=v_raw[:, PAIR * j + n].rearrange("p j d -> p d j"),
+                    start=True,
+                    stop=True,
+                )
+            v_flipped[j] = flipped
+
+        def copy_values(j):
+            nc.scalar.copy(out=v_grouped[:, PAIR * j : PAIR * (j + 1)], in_=v_flipped[j][:])
+
         def regroup_values(copy, i):
             copy(
                 out=v_grouped[:, i].rearrange("p (c i) j -> p c j i", i=4),
@@ -147,6 +164,7 @@ def tile_mhla2_pa_kernel(tc, x_k, W_K, v_heads, out):
             )
 
         k_banks, shifts, exps, row_sums, inv_sums, p_groupeds, o_banks = {}, {}, {}, {}, {}, {}, {}
+        v_flipped = {}
 
         def project(i):
             b, h = divmod(i, H)
@@ -241,26 +259,25 @@ def tile_mhla2_pa_kernel(tc, x_k, W_K, v_heads, out):
             )
 
         regroup_weights_vector(0)
-        regroup_weights_scalar(1)
         quantise_weights(0, 1)
         for t in range(PACK):
             transpose_tokens(t)
-        quantise_weights(1, 1)
+        regroup_weights_vector(1)
         quantise_tokens(0)
-        regroup_weights_vector(2)
+        quantise_weights(1, 1)
         quantise_tokens(1)
         quantise_tokens(2)
-        quantise_weights(2, 1)
+        regroup_weights_vector(2)
         quantise_tokens(3)
         project(0)
-        regroup_weights_vector(3)
-        regroup_values(nc.scalar.copy, 0)
-        regroup_values(nc.scalar.copy, 1)
+        regroup_weights_scalar(3)
+        quantise_weights(2, 1)
         maxima(0)
         shift_scale(0)
         project(1)
         maxima(1)
         quantise_weights(3, 1)
+        flip_values(0)
         LAST = BANKS - 1
         for i in range(BANKS + 3):
             j, n = divmod(i, PAIR)
@@ -279,24 +296,28 @@ def tile_mhla2_pa_kernel(tc, x_k, W_K, v_heads, out):
                 normalise(i - PAIR, PAIR)
             if LAST <= i <= LAST + 1:
                 normalise(i - 1, 1)
-            if 3 <= i < 7:
-                quantise_tokens(i + 1)
+            if 2 <= i < 6:
+                quantise_tokens(i + 2)
+            if i == 0:
+                copy_values(0)
             if i + 2 < BANKS:
                 project(i + 2)
             if i in (0, 1):
                 regroup_weights_vector(4 + 2 * i)
+            if i == 0:
                 regroup_weights_scalar(5 + 2 * i)
+            if i == 1:
+                regroup_weights_vector(5 + 2 * i)
             if i in (1, 3):
                 quantise_weights(i + 3, 2)
-            if 2 <= i < BANKS - 1:
-                if i in (9, 11, 13):
-                    regroup_values(nc.vector.tensor_copy, i)
-                else:
-                    regroup_values(nc.scalar.copy, i)
-                if i == BANKS - 2:
-                    regroup_values(nc.vector.tensor_copy, i + 1)
-            if 2 <= i < 6:
-                transpose_tokens(i + 2)
+            if 1 <= i < 5:
+                transpose_tokens(i + 3)
+            if n == 0 and 1 <= j < BANKS // PAIR - 1:
+                flip_values(j)
+            if n == 1 and 1 <= j < BANKS // PAIR - 1:
+                copy_values(j)
+            if BANKS - 4 <= i < BANKS - 2:
+                regroup_values(nc.vector.tensor_copy, i + 2)
             if n == 1 and 1 <= j <= BANKS // PAIR:
                 if j < BANKS // PAIR:
                     quantise_values(PAIR * (j - 1), PAIR)

@@ -195,11 +195,11 @@ def tile_mhla2_pa_kernel(tc, x_k, W_K, v_heads, out):
             j, n = divmod(i, PAIR)
             shift = shifts[i]
             if n == 0:
-                exps[j] = ring.tile([P, PAIR, PACK, DH], F32, name="e")
+                exps[j] = ring.tile([P, PACK, PAIR, DH], F32, name="e")
                 row_sums[j] = ring.tile([P, PAIR, PACK], F32, name="row_sum")
             for t in range(PACK):
                 nc.scalar.activation(
-                    out=exps[j][:, n, t, :],
+                    out=exps[j][:, t, n, :],
                     in_=k_banks[i][:, t, :],
                     func=ACT.Exp,
                     bias=shift[:, t : t + 1],
@@ -210,18 +210,21 @@ def tile_mhla2_pa_kernel(tc, x_k, W_K, v_heads, out):
         def invert_sums(i0, n):
             j, n0 = divmod(i0, PAIR)
             if n0 == 0:
-                inv_sums[j] = ring.tile([P, PAIR, PACK], F32, name="inv_sum")
+                inv_sums[j] = ring.tile([P, PAIR, PACK, 4], F32, name="inv_sum")
                 p_groupeds[j] = ring.tile([P, PAIR, DH, PACK], BF16, name="p_grouped", align_bytes=64)
             nc.vector.reciprocal(
-                out=inv_sums[j][:, n0 : n0 + n], in_=row_sums[j][:, n0 : n0 + n]
+                out=inv_sums[j][:, n0 : n0 + n],
+                in_=row_sums[j][:, n0 : n0 + n].unsqueeze(3).to_broadcast([P, n, PACK, 4]),
             )
 
         def normalise(i0, n):
             j, n0 = divmod(i0, PAIR)
             nc.vector.tensor_tensor(
-                out=p_groupeds[j][:, n0 : n0 + n],
-                in0=exps[j][:, n0 : n0 + n].rearrange("p n t d -> p n d t"),
-                in1=inv_sums[j][:, n0 : n0 + n].unsqueeze(2).to_broadcast([P, n, DH, PACK]),
+                out=p_groupeds[j][:, n0 : n0 + n].rearrange("p n (c i) t -> p n c t i", i=4),
+                in0=exps[j][:, :, n0 : n0 + n].rearrange("p t n (c i) -> p n c t i", i=4),
+                in1=inv_sums[j][:, n0 : n0 + n]
+                .unsqueeze(2)
+                .to_broadcast([P, n, DH // 4, PACK, 4]),
                 op=ALU.mult,
             )
 

@@ -69,16 +69,16 @@ def tile_mhla2_pa_kernel(tc, x_k, W_K, v_heads, out):
             )
 
         load_weights(0, 1)
-        load_tokens(0, 0)
         load_weights(1, 1)
+        load_tokens(0, 0)
+        load_weights(2, 1)
         load_tokens(0, 1)
         load_tokens(0, 2)
-        load_tokens(0, 3)
-        load_weights(2, 1)
         load_weights(3, 1)
+        load_tokens(0, 3)
         load_weights(4, 1)
-        load_values(0, 0, 2)
         load_weights(5, 1)
+        load_values(0, 0, 2)
         load_weights(6, 2)
         for t in range(PACK):
             load_tokens(1, t)
@@ -164,7 +164,7 @@ def tile_mhla2_pa_kernel(tc, x_k, W_K, v_heads, out):
             )
 
         k_banks, shifts, exps, row_sums, inv_sums, p_groupeds, o_banks = {}, {}, {}, {}, {}, {}, {}
-        v_flipped = {}
+        v_flipped, inv_runs = {}, {}
 
         def project(i):
             b, h = divmod(i, H)
@@ -210,23 +210,32 @@ def tile_mhla2_pa_kernel(tc, x_k, W_K, v_heads, out):
         def invert_sums(i0, n):
             j, n0 = divmod(i0, PAIR)
             if n0 == 0:
-                inv_sums[j] = ring.tile([P, PAIR, PACK, 4], F32, name="inv_sum")
+                inv_sums[j] = ring.tile([P, PAIR, PACK], F32, name="inv_sum")
+                inv_runs[j] = ring.tile([P, PAIR, PACK, 4], F32, name="inv_run")
                 p_groupeds[j] = ring.tile([P, PAIR, DH, PACK], BF16, name="p_grouped", align_bytes=64)
             nc.vector.reciprocal(
-                out=inv_sums[j][:, n0 : n0 + n],
-                in_=row_sums[j][:, n0 : n0 + n].unsqueeze(3).to_broadcast([P, n, PACK, 4]),
+                out=inv_sums[j][:, n0 : n0 + n], in_=row_sums[j][:, n0 : n0 + n]
+            )
+            if n == 1:
+                return
+            nc.gpsimd.tensor_copy(
+                out=inv_runs[j][:, n0 : n0 + n],
+                in_=inv_sums[j][:, n0 : n0 + n].unsqueeze(3).to_broadcast([P, n, PACK, 4]),
             )
 
         def normalise(i0, n):
             j, n0 = divmod(i0, PAIR)
-            nc.vector.tensor_tensor(
-                out=p_groupeds[j][:, n0 : n0 + n].rearrange("p n (c i) t -> p n c t i", i=4),
-                in0=exps[j][:, :, n0 : n0 + n].rearrange("p t n (c i) -> p n c t i", i=4),
-                in1=inv_sums[j][:, n0 : n0 + n]
-                .unsqueeze(2)
-                .to_broadcast([P, n, DH // 4, PACK, 4]),
-                op=ALU.mult,
-            )
+            if n == PAIR:
+                out_view = p_groupeds[j][:].rearrange("p n (c i) t -> p n c t i", i=4)
+                e_view = exps[j][:].rearrange("p t n (c i) -> p n c t i", i=4)
+                inv_view = inv_runs[j][:].unsqueeze(2).to_broadcast([P, PAIR, DH // 4, PACK, 4])
+            else:
+                out_view = p_groupeds[j][:, n0].rearrange("p (c i) t -> p c t i", i=4)
+                e_view = exps[j][:, :, n0].rearrange("p t (c i) -> p c t i", i=4)
+                inv_view = (
+                    inv_sums[j][:, n0].unsqueeze(1).unsqueeze(3).to_broadcast([P, DH // 4, PACK, 4])
+                )
+            nc.vector.tensor_tensor(out=out_view, in0=e_view, in1=inv_view, op=ALU.mult)
 
         def quantise_probabilities(i0, n):
             j, n0 = divmod(i0, PAIR)
@@ -262,24 +271,27 @@ def tile_mhla2_pa_kernel(tc, x_k, W_K, v_heads, out):
             )
 
         regroup_weights_vector(0)
+        regroup_weights_scalar(1)
         quantise_weights(0, 1)
+        regroup_weights_vector(2)
         for t in range(PACK):
             transpose_tokens(t)
-        regroup_weights_vector(1)
-        quantise_tokens(0)
         quantise_weights(1, 1)
+        quantise_weights(2, 1)
+        quantise_tokens(0)
+        regroup_weights_vector(3)
         quantise_tokens(1)
         quantise_tokens(2)
-        regroup_weights_vector(2)
+        quantise_weights(3, 1)
+        regroup_weights_vector(4)
+        regroup_weights_scalar(5)
         quantise_tokens(3)
         project(0)
-        regroup_weights_scalar(3)
-        quantise_weights(2, 1)
+        project(1)
+        quantise_weights(4, 1)
         maxima(0)
         shift_scale(0)
-        project(1)
         maxima(1)
-        quantise_weights(3, 1)
         flip_values(0)
         LAST = BANKS - 1
         for i in range(BANKS + 3):
@@ -305,22 +317,21 @@ def tile_mhla2_pa_kernel(tc, x_k, W_K, v_heads, out):
                 copy_values(0)
             if i + 2 < BANKS:
                 project(i + 2)
-            if i in (0, 1):
-                regroup_weights_vector(4 + 2 * i)
             if i == 0:
-                regroup_weights_scalar(5 + 2 * i)
+                regroup_weights_vector(6)
+                quantise_weights(5, 1)
             if i == 1:
-                regroup_weights_vector(5 + 2 * i)
-            if i in (1, 3):
-                quantise_weights(i + 3, 2)
+                regroup_weights_vector(7)
+            if i == 2:
+                quantise_weights(6, 2)
             if 1 <= i < 5:
                 transpose_tokens(i + 3)
-            if n == 0 and 1 <= j < BANKS // PAIR - 1:
+            if n == 0 and 1 <= j < 7:
                 flip_values(j)
-            if n == 1 and 1 <= j < BANKS // PAIR - 1:
+            if n == 1 and 1 <= j < 7:
                 copy_values(j)
-            if BANKS - 4 <= i < BANKS - 2:
-                regroup_values(nc.vector.tensor_copy, i + 2)
+            if 10 <= i < 12:
+                regroup_values(nc.scalar.copy, i + 4)
             if n == 1 and 1 <= j <= BANKS // PAIR:
                 if j < BANKS // PAIR:
                     quantise_values(PAIR * (j - 1), PAIR)

@@ -68,21 +68,23 @@ def tile_mhla2_pa_kernel(tc, x_k, W_K, v_heads, out):
                 in_=v_heads[b, h0 : h0 + heads].rearrange("h (p t) e -> p h t e", t=PACK),
             )
 
-        load_weights(0, 1)
-        load_weights(1, 1)
         load_tokens(0, 0)
-        load_weights(2, 1)
         load_tokens(0, 1)
+        load_weights(0, 1)
         load_tokens(0, 2)
-        load_weights(3, 1)
         load_tokens(0, 3)
+        load_weights(1, 1)
+        load_weights(2, 1)
+        load_weights(3, 1)
         load_weights(4, 1)
         load_weights(5, 1)
-        load_values(0, 0, 2)
+        load_tokens(1, 0)
+        load_tokens(1, 1)
         load_weights(6, 2)
-        for t in range(PACK):
-            load_tokens(1, t)
-        load_values(0, 2, 6)
+        load_values(0, 0, 4)
+        load_tokens(1, 2)
+        load_tokens(1, 3)
+        load_values(0, 4, 4)
         load_values(1, 0, 8)
 
         identity = keep.tile([P, P], F32)
@@ -94,22 +96,28 @@ def tile_mhla2_pa_kernel(tc, x_k, W_K, v_heads, out):
         nc.vector.memset(warm[:], 0.0)
         nc.scalar.activation(out=warm[:], in_=warm[:], func=ACT.Exp)
 
+        x_flipped = {}
+
         def transpose_tokens(tt):
             words = x_raw[:, tt, :].bitcast(F32).rearrange("p (g q u) -> p g u q", g=G, u=2)
             flipped = psum_x.tile([P, G, 2, P], F32, name="flipped")
             for g in range(G):
                 for u in range(2):
                     nc.tensor.transpose(flipped[:, g, u, :], words[:, g, u, :], identity[:])
+            x_flipped[tt] = flipped
+
+        def copy_tokens(tt):
+            flipped = x_flipped[tt]
             nc.scalar.copy(
                 out=x_grouped[:, tt].bitcast(F32).rearrange("p g (n u) -> p g n u", u=2),
                 in_=flipped[:].rearrange("p g u n -> p g n u"),
             )
 
-        def quantise_tokens(tt):
+        def quantise_tokens(tt, n):
             nc.vector.quantize_mx(
-                out=x_codes[:, tt].rearrange("p g n -> p (g n)").bitcast(FP8X4),
-                scales=x_scales[:, tt].rearrange("p g n -> p (g n)"),
-                in_=x_grouped[:, tt].rearrange("p g c -> p (g c)"),
+                out=x_codes[:, tt : tt + n].rearrange("p s g n -> p (s g n)").bitcast(FP8X4),
+                scales=x_scales[:, tt : tt + n].rearrange("p s g n -> p (s g n)"),
+                in_=x_grouped[:, tt : tt + n].rearrange("p s g c -> p (s g c)"),
             )
 
         def regroup_weights_vector(h):
@@ -271,78 +279,74 @@ def tile_mhla2_pa_kernel(tc, x_k, W_K, v_heads, out):
             )
 
         regroup_weights_vector(0)
-        regroup_weights_scalar(1)
-        quantise_weights(0, 1)
-        regroup_weights_vector(2)
         for t in range(PACK):
             transpose_tokens(t)
-        quantise_weights(1, 1)
-        quantise_weights(2, 1)
-        quantise_tokens(0)
-        regroup_weights_vector(3)
-        quantise_tokens(1)
-        quantise_tokens(2)
-        quantise_weights(3, 1)
-        regroup_weights_vector(4)
-        regroup_weights_scalar(5)
-        quantise_tokens(3)
+            copy_tokens(t)
+        quantise_weights(0, 1)
+        quantise_tokens(0, 2)
+        regroup_weights_vector(1)
+        regroup_weights_scalar(2)
+        quantise_tokens(2, 2)
         project(0)
+        quantise_weights(1, 1)
+        regroup_weights_vector(3)
+        regroup_weights_scalar(4)
         project(1)
-        quantise_weights(4, 1)
+        quantise_weights(2, 1)
         maxima(0)
         shift_scale(0)
+        project(2)
         maxima(1)
-        flip_values(0)
+        regroup_weights_vector(5)
+        quantise_weights(3, 1)
         LAST = BANKS - 1
-        for i in range(BANKS + 3):
+        for i in range(BANKS + 5):
             j, n = divmod(i, PAIR)
-            if i < BANKS:
-                exponentials(i)
-            if n == 0 and 1 <= j < BANKS // PAIR:
-                invert_sums(i - PAIR, PAIR)
-            if i >= LAST:
-                if i <= LAST + 1:
-                    invert_sums(i - 1, 1)
-            if 1 <= i and i + 1 < BANKS:
-                maxima(i + 1)
+            if i + 3 < BANKS and n == 1:
+                project(i + 3)
             if i + 1 < BANKS:
                 shift_scale(i + 1)
-            if n == 0 and 1 <= j < BANKS // PAIR:
-                normalise(i - PAIR, PAIR)
-            if LAST <= i <= LAST + 1:
-                normalise(i - 1, 1)
-            if 2 <= i < 6:
-                quantise_tokens(i + 2)
-            if i == 0:
-                copy_values(0)
             if i + 2 < BANKS:
-                project(i + 2)
+                maxima(i + 2)
+            if n == 1 and 1 <= j < BANKS // PAIR:
+                normalise(i - 3, PAIR)
+            if i < BANKS:
+                exponentials(i)
             if i == 0:
+                quantise_weights(4, 2)
                 regroup_weights_vector(6)
-                quantise_weights(5, 1)
-            if i == 1:
                 regroup_weights_vector(7)
             if i == 2:
                 quantise_weights(6, 2)
-            if 1 <= i < 5:
-                transpose_tokens(i + 3)
-            if n == 0 and 1 <= j < 7:
-                flip_values(j)
-            if n == 1 and 1 <= j < 7:
-                copy_values(j)
-            if 10 <= i < 12:
-                regroup_values(nc.scalar.copy, i + 4)
-            if n == 1 and 1 <= j <= BANKS // PAIR:
-                if j < BANKS // PAIR:
-                    quantise_values(PAIR * (j - 1), PAIR)
-                    quantise_probabilities(i - 1 - PAIR, PAIR)
-                    summarise(i - 1 - PAIR, PAIR)
-            if i == LAST:
-                quantise_values(BANKS - PAIR, PAIR)
-            if LAST <= i <= LAST + 1:
-                quantise_probabilities(i - 1, 1)
-                summarise(i - 1, 1)
+            if n == 0 and 1 <= j < BANKS // PAIR:
+                invert_sums(i - 2, PAIR)
+            if 15 <= i <= 16:
+                invert_sums(i - 1, 1)
+            if 16 <= i <= 17:
+                normalise(i - 2, 1)
+            if i < 4:
+                transpose_tokens(PACK + i)
+                copy_tokens(PACK + i)
+            if i + 3 < BANKS and n == 0:
+                project(i + 3)
+            if i in (2, 4):
+                quantise_tokens(PACK + i - 2, 2)
+            if n == 0 and 1 <= j <= BANKS // PAIR:
+                quantise_values(i - 2, PAIR)
             if n == 0 and 2 <= j <= BANKS // PAIR:
-                store(i - 2 * PAIR, PAIR)
-            if LAST + 1 <= i <= LAST + 2:
-                store(i - 2, 1)
+                quantise_probabilities(i - 4, PAIR)
+            if n == 1 and 2 <= j <= BANKS // PAIR:
+                summarise(i - 5, PAIR)
+            if 17 <= i <= 18:
+                quantise_probabilities(i - 3, 1)
+                summarise(i - 3, 1)
+            if i < 2:
+                regroup_values(nc.scalar.copy, i)
+            if n == 0 and 1 <= j < BANKS // PAIR:
+                copy_values(j)
+            if n == 1 and j < BANKS // PAIR - 1:
+                flip_values(j + 1)
+            if n == 0 and 3 <= j < BANKS // PAIR + 2:
+                store(i - 6, PAIR)
+            if 18 <= i <= 19:
+                store(i - 4, 1)

@@ -172,7 +172,7 @@ def tile_mhla2_pa_kernel(tc, x_k, W_K, v_heads, out):
             )
 
         k_banks, shifts, exps, row_sums, inv_sums, p_groupeds, o_banks = {}, {}, {}, {}, {}, {}, {}
-        v_flipped, inv_runs = {}, {}
+        v_flipped = {}
 
         def project(i):
             b, h = divmod(i, H)
@@ -219,31 +219,20 @@ def tile_mhla2_pa_kernel(tc, x_k, W_K, v_heads, out):
             j, n0 = divmod(i0, PAIR)
             if n0 == 0:
                 inv_sums[j] = ring.tile([P, PAIR, PACK], F32, name="inv_sum")
-                inv_runs[j] = ring.tile([P, PAIR, PACK, 4], F32, name="inv_run")
                 p_groupeds[j] = ring.tile([P, PAIR, DH, PACK], BF16, name="p_grouped", align_bytes=64)
             nc.vector.reciprocal(
                 out=inv_sums[j][:, n0 : n0 + n], in_=row_sums[j][:, n0 : n0 + n]
             )
-            if n == 1:
-                return
-            nc.gpsimd.tensor_copy(
-                out=inv_runs[j][:, n0 : n0 + n],
-                in_=inv_sums[j][:, n0 : n0 + n].unsqueeze(3).to_broadcast([P, n, PACK, 4]),
-            )
 
         def normalise(i0, n):
             j, n0 = divmod(i0, PAIR)
-            if n == PAIR:
-                out_view = p_groupeds[j][:].rearrange("p n (c i) t -> p n c t i", i=4)
-                e_view = exps[j][:].rearrange("p t n (c i) -> p n c t i", i=4)
-                inv_view = inv_runs[j][:].unsqueeze(2).to_broadcast([P, PAIR, DH // 4, PACK, 4])
-            else:
-                out_view = p_groupeds[j][:, n0].rearrange("p (c i) t -> p c t i", i=4)
-                e_view = exps[j][:, :, n0].rearrange("p t (c i) -> p c t i", i=4)
-                inv_view = (
-                    inv_sums[j][:, n0].unsqueeze(1).unsqueeze(3).to_broadcast([P, DH // 4, PACK, 4])
+            for m in range(n0, n0 + n):
+                nc.vector.tensor_tensor(
+                    out=p_groupeds[j][:, m].rearrange("p (c i) t -> p c t i", i=4),
+                    in0=exps[j][:, :, m].rearrange("p t (c i) -> p c t i", i=4),
+                    in1=inv_sums[j][:, m].unsqueeze(1).unsqueeze(3).to_broadcast([P, DH // 4, PACK, 4]),
+                    op=ALU.mult,
                 )
-            nc.vector.tensor_tensor(out=out_view, in0=e_view, in1=inv_view, op=ALU.mult)
 
         def quantise_probabilities(i0, n):
             j, n0 = divmod(i0, PAIR)
@@ -297,7 +286,7 @@ def tile_mhla2_pa_kernel(tc, x_k, W_K, v_heads, out):
         shift_scale(0)
         project(2)
         maxima(1)
-        regroup_weights_vector(5)
+        regroup_weights_scalar(5)
         quantise_weights(3, 1)
         LAST = BANKS - 1
         for i in range(BANKS + 5):
@@ -341,7 +330,7 @@ def tile_mhla2_pa_kernel(tc, x_k, W_K, v_heads, out):
                 quantise_probabilities(i - 3, 1)
                 summarise(i - 3, 1)
             if i < 2:
-                regroup_values(nc.scalar.copy, i)
+                regroup_values(nc.vector.tensor_copy, i)
             if n == 0 and 1 <= j < BANKS // PAIR:
                 copy_values(j)
             if n == 1 and j < BANKS // PAIR - 1:

@@ -74,15 +74,15 @@ def tile_mhla2_pa_kernel(tc, x_k, W_K, v_heads, out):
         load_tokens(0, 2)
         load_tokens(0, 3)
         load_weights(1, 1)
+        load_weights(4, 1)
         load_weights(2, 1)
         load_weights(3, 1)
-        load_weights(4, 1)
         load_weights(5, 1)
         load_tokens(1, 0)
-        load_tokens(1, 1)
         load_weights(6, 2)
-        load_values(0, 0, 4)
+        load_tokens(1, 1)
         load_tokens(1, 2)
+        load_values(0, 0, 4)
         load_tokens(1, 3)
         load_values(0, 4, 4)
         load_values(1, 0, 8)
@@ -273,69 +273,83 @@ def tile_mhla2_pa_kernel(tc, x_k, W_K, v_heads, out):
             copy_tokens(t)
         quantise_weights(0, 1)
         quantise_tokens(0, 2)
-        regroup_weights_vector(1)
-        regroup_weights_scalar(2)
-        quantise_tokens(2, 2)
-        project(0)
-        quantise_weights(1, 1)
-        regroup_weights_vector(3)
         regroup_weights_scalar(4)
+        regroup_weights_vector(1)
+        regroup_weights_scalar(3)
+        quantise_tokens(2, 1)
+        regroup_weights_scalar(5)
+        quantise_weights(1, 1)
+        quantise_tokens(3, 1)
+        regroup_weights_vector(2)
+        project(0)
         project(1)
+        quantise_weights(4, 1)
         quantise_weights(2, 1)
         maxima(0)
-        shift_scale(0)
-        project(2)
         maxima(1)
-        regroup_weights_scalar(5)
+        project(2)
+        shift_scale(0)
         quantise_weights(3, 1)
         LAST = BANKS - 1
-        for i in range(BANKS + 5):
+        for i in range(BANKS + 6):
             j, n = divmod(i, PAIR)
-            if i + 3 < BANKS and n == 1:
+            if n == 1 and i < 4:
+                transpose_tokens(PACK + i)
+            if n == 1 and 2 <= j <= BANKS // PAIR:
+                summarise(i - 5, PAIR)
+            if 2 <= i < 6:
+                quantise_tokens(i + 2, 1)
+            if n == 1 and i + 3 < BANKS:
                 project(i + 3)
-            if i + 1 < BANKS:
+            if n == 0 and i + 1 < BANKS:
                 shift_scale(i + 1)
+            if i == 0:
+                regroup_weights_vector(6)
+                regroup_weights_vector(7)
+            if i < BANKS:
+                exponentials(i)
+            if n == 1 and i + 1 < BANKS:
+                shift_scale(i + 1)
+            if n == 0 and 1 <= j < BANKS // PAIR:
+                copy_values(j - 1)
+            if i in (5, 7):
+                regroup_values(nc.scalar.copy, BANKS - PAIR + i // 7)
+            if n == 1 and i < 4:
+                copy_tokens(PACK + i)
+            if n == 0 and i < 4:
+                transpose_tokens(PACK + i)
+            if n == 1 and j < BANKS // PAIR - 1:
+                flip_values(j)
+            if n == 0 and i + 3 < BANKS:
+                project(i + 3)
+            if n == 1 and 1 <= j < BANKS // PAIR:
+                normalise(i - 3, PAIR)
             if i + 2 < BANKS:
                 maxima(i + 2)
             if n == 1 and 1 <= j < BANKS // PAIR:
-                normalise(i - 3, PAIR)
-            if i < BANKS:
-                exponentials(i)
-            if i == 0:
-                quantise_weights(4, 2)
-                regroup_weights_vector(6)
-                regroup_weights_vector(7)
-            if i == 2:
-                quantise_weights(6, 2)
+                quantise_values(i - 3, PAIR)
+            if i == LAST:
+                quantise_values(BANKS - PAIR, PAIR)
             if n == 0 and 1 <= j < BANKS // PAIR:
                 invert_sums(i - 2, PAIR)
-            if 15 <= i <= 16:
-                invert_sums(i - 1, 1)
+            if i == LAST:
+                invert_sums(LAST - 1, 1)
+            if i == 0:
+                quantise_weights(5, 1)
+            if i == 2:
+                quantise_weights(6, 2)
+            if n == 0 and i < 4:
+                copy_tokens(PACK + i)
             if 16 <= i <= 17:
                 normalise(i - 2, 1)
-            if i < 4:
-                transpose_tokens(PACK + i)
-                copy_tokens(PACK + i)
-            if i + 3 < BANKS and n == 0:
-                project(i + 3)
-            if i in (2, 4):
-                quantise_tokens(PACK + i - 2, 2)
-            if n == 0 and 1 <= j <= BANKS // PAIR:
-                quantise_values(i - 2, PAIR)
             if n == 0 and 2 <= j <= BANKS // PAIR:
                 quantise_probabilities(i - 4, PAIR)
-            if n == 1 and 2 <= j <= BANKS // PAIR:
-                summarise(i - 5, PAIR)
+            if i == BANKS:
+                invert_sums(LAST, 1)
             if 17 <= i <= 18:
                 quantise_probabilities(i - 3, 1)
                 summarise(i - 3, 1)
-            if i < 2:
-                regroup_values(nc.vector.tensor_copy, i)
-            if n == 0 and 1 <= j < BANKS // PAIR:
-                copy_values(j)
-            if n == 1 and j < BANKS // PAIR - 1:
-                flip_values(j + 1)
-            if n == 0 and 3 <= j < BANKS // PAIR + 2:
+            if n == 0 and 3 <= j < BANKS // PAIR + 3 - 1:
                 store(i - 6, PAIR)
             if 18 <= i <= 19:
                 store(i - 4, 1)

@@ -123,8 +123,8 @@ def tile_mhla2_pa_kernel(tc, x_k, W_K, v_heads, out):
         def regroup_weights_vector(h):
             slabs = slice(h * G, (h + 1) * G)
             nc.vector.tensor_copy(
-                out=w_grouped[:, slabs].rearrange("p s (c i) j -> p s c j i", i=4),
-                in_=w_raw[:, slabs].rearrange("p s j (c i) -> p s c j i", i=4),
+                out=w_grouped[:, slabs].rearrange("p s (c i) j -> p s c j i", i=8),
+                in_=w_raw[:, slabs].rearrange("p s j (c i) -> p s c j i", i=8),
             )
 
         def regroup_weights_scalar(h):

@@ -87,6 +87,7 @@ def tile_mhla2_pa_kernel(tc, x_k, W_K, v_heads, out):
         load_values(0, 4, 4)
         load_values(1, 0, 8)
 
+
         identity = keep.tile([P, P], F32)
         make_identity(nc, identity[:])
         identity_bf16 = keep.tile([P, P], BF16)
@@ -203,11 +204,11 @@ def tile_mhla2_pa_kernel(tc, x_k, W_K, v_heads, out):
             j, n = divmod(i, PAIR)
             shift = shifts[i]
             if n == 0:
-                exps[j] = ring.tile([P, PACK, PAIR, DH], F32, name="e")
+                exps[j] = ring.tile([P, PAIR, PACK, DH], F32, name="e")
                 row_sums[j] = ring.tile([P, PAIR, PACK], F32, name="row_sum")
             for t in range(PACK):
                 nc.scalar.activation(
-                    out=exps[j][:, t, n, :],
+                    out=exps[j][:, n, t, :],
                     in_=k_banks[i][:, t, :],
                     func=ACT.Exp,
                     bias=shift[:, t : t + 1],
@@ -229,7 +230,7 @@ def tile_mhla2_pa_kernel(tc, x_k, W_K, v_heads, out):
             for m in range(n0, n0 + n):
                 nc.vector.tensor_tensor(
                     out=p_groupeds[j][:, m].rearrange("p (c i) t -> p c t i", i=4),
-                    in0=exps[j][:, :, m].rearrange("p t (c i) -> p c t i", i=4),
+                    in0=exps[j][:, m].rearrange("p t (c i) -> p c t i", i=4),
                     in1=inv_sums[j][:, m].unsqueeze(1).unsqueeze(3).to_broadcast([P, DH // 4, PACK, 4]),
                     op=ALU.mult,
                 )
@@ -328,24 +329,24 @@ def tile_mhla2_pa_kernel(tc, x_k, W_K, v_heads, out):
                 maxima(i + 2)
             if n == 1 and 1 <= j < BANKS // PAIR:
                 quantise_values(i - 3, PAIR)
-            if i == LAST:
-                quantise_values(BANKS - PAIR, PAIR)
             if n == 0 and 1 <= j < BANKS // PAIR:
                 invert_sums(i - 2, PAIR)
             if i == LAST:
                 invert_sums(LAST - 1, 1)
+                quantise_values(BANKS - PAIR, PAIR)
             if i == 0:
                 quantise_weights(5, 1)
             if i == 2:
                 quantise_weights(6, 2)
             if n == 0 and i < 4:
                 copy_tokens(PACK + i)
-            if 16 <= i <= 17:
-                normalise(i - 2, 1)
+            if i == BANKS:
+                normalise(LAST - 1, 1)
+                invert_sums(LAST, 1)
             if n == 0 and 2 <= j <= BANKS // PAIR:
                 quantise_probabilities(i - 4, PAIR)
-            if i == BANKS:
-                invert_sums(LAST, 1)
+            if i == BANKS + 1:
+                normalise(LAST, 1)
             if 17 <= i <= 18:
                 quantise_probabilities(i - 3, 1)
                 summarise(i - 3, 1)

@@ -158,8 +158,8 @@ def tile_mhla2_pa_kernel(tc, x_k, W_K, v_heads, out):
         def copy_values(j):
             nc.scalar.copy(out=v_grouped[:, PAIR * j : PAIR * (j + 1)], in_=v_flipped[j][:])
 
-        def regroup_values(copy, i):
-            copy(
+        def regroup_values(i):
+            nc.scalar.copy(
                 out=v_grouped[:, i].rearrange("p (c i) j -> p c j i", i=4),
                 in_=v_raw[:, i].rearrange("p j (c i) -> p c j i", i=4),
             )
@@ -172,7 +172,7 @@ def tile_mhla2_pa_kernel(tc, x_k, W_K, v_heads, out):
                 in_=v_grouped[:, banks].rearrange("p s d j -> p (s d j)"),
             )
 
-        k_banks, shifts, exps, row_sums, inv_sums, p_groupeds, o_banks = {}, {}, {}, {}, {}, {}, {}
+        k_banks, row_maxes, shifts, exps, row_sums, inv_sums, p_groupeds, o_banks = {}, {}, {}, {}, {}, {}, {}, {}
         v_flipped = {}
 
         def project(i):
@@ -191,18 +191,19 @@ def tile_mhla2_pa_kernel(tc, x_k, W_K, v_heads, out):
                     )
 
         def maxima(i):
-            row_max = ring.tile([P, PACK], F32, name="row_max")
-            nc.vector.tensor_reduce(out=row_max[:], in_=k_banks[i][:], axis=AXIS.X, op=ALU.max)
-            shifts[i] = row_max
+            j, n = divmod(i, PAIR)
+            if n == 0:
+                row_maxes[j] = ring.tile([P, PAIR, PACK], F32, name="row_max")
+            nc.vector.tensor_reduce(
+                out=row_maxes[j][:, n], in_=k_banks[i][:], axis=AXIS.X, op=ALU.max
+            )
 
-        def shift_scale(i):
-            shift = ring.tile([P, PACK], F32, name="shift")
-            nc.scalar.mul(out=shift[:], in_=shifts[i][:], mul=-SOFTMAX_SCALE)
-            shifts[i] = shift
+        def shift_scale(j):
+            shifts[j] = ring.tile([P, PAIR, PACK], F32, name="shift")
+            nc.scalar.mul(out=shifts[j][:], in_=row_maxes[j][:], mul=-SOFTMAX_SCALE)
 
         def exponentials(i):
             j, n = divmod(i, PAIR)
-            shift = shifts[i]
             if n == 0:
                 exps[j] = ring.tile([P, PAIR, PACK, DH], F32, name="e")
                 row_sums[j] = ring.tile([P, PAIR, PACK], F32, name="row_sum")
@@ -211,7 +212,7 @@ def tile_mhla2_pa_kernel(tc, x_k, W_K, v_heads, out):
                     out=exps[j][:, n, t, :],
                     in_=k_banks[i][:, t, :],
                     func=ACT.Exp,
-                    bias=shift[:, t : t + 1],
+                    bias=shifts[j][:, n, t : t + 1],
                     scale=SOFTMAX_SCALE,
                     accum_out=row_sums[j][:, n, t : t + 1],
                 )
@@ -225,15 +226,15 @@ def tile_mhla2_pa_kernel(tc, x_k, W_K, v_heads, out):
                 out=inv_sums[j][:, n0 : n0 + n], in_=row_sums[j][:, n0 : n0 + n]
             )
 
-        def normalise(i0, n):
-            j, n0 = divmod(i0, PAIR)
-            for m in range(n0, n0 + n):
-                nc.vector.tensor_tensor(
-                    out=p_groupeds[j][:, m].rearrange("p (c i) t -> p c t i", i=4),
-                    in0=exps[j][:, m].rearrange("p t (c i) -> p c t i", i=4),
-                    in1=inv_sums[j][:, m].unsqueeze(1).unsqueeze(3).to_broadcast([P, DH // 4, PACK, 4]),
-                    op=ALU.mult,
-                )
+        def normalise(engine, i, d0, width):
+            j, n = divmod(i, PAIR)
+            features = slice(d0, d0 + width)
+            engine.tensor_tensor(
+                out=p_groupeds[j][:, n, features].rearrange("p (c i) t -> p c t i", i=4),
+                in0=exps[j][:, n, :, features].rearrange("p t (c i) -> p c t i", i=4),
+                in1=inv_sums[j][:, n].unsqueeze(1).unsqueeze(3).to_broadcast([P, width // 4, PACK, 4]),
+                op=ALU.mult,
+            )
 
         def quantise_probabilities(i0, n):
             j, n0 = divmod(i0, PAIR)
@@ -272,8 +273,9 @@ def tile_mhla2_pa_kernel(tc, x_k, W_K, v_heads, out):
         for t in range(PACK):
             transpose_tokens(t)
             copy_tokens(t)
+        quantise_tokens(0, 1)
         quantise_weights(0, 1)
-        quantise_tokens(0, 2)
+        quantise_tokens(1, 1)
         regroup_weights_scalar(4)
         regroup_weights_vector(1)
         regroup_weights_scalar(3)
@@ -284,73 +286,80 @@ def tile_mhla2_pa_kernel(tc, x_k, W_K, v_heads, out):
         regroup_weights_vector(2)
         project(0)
         project(1)
+        transpose_tokens(4)
         quantise_weights(4, 1)
         quantise_weights(2, 1)
         maxima(0)
         maxima(1)
-        project(2)
         shift_scale(0)
+        copy_tokens(4)
+        project(2)
         quantise_weights(3, 1)
-        LAST = BANKS - 1
-        for i in range(BANKS + 6):
-            j, n = divmod(i, PAIR)
-            if n == 1 and i < 4:
-                transpose_tokens(PACK + i)
-            if n == 1 and 2 <= j <= BANKS // PAIR:
-                summarise(i - 5, PAIR)
-            if 2 <= i < 6:
-                quantise_tokens(i + 2, 1)
-            if n == 1 and i + 3 < BANKS:
-                project(i + 3)
-            if n == 0 and i + 1 < BANKS:
-                shift_scale(i + 1)
-            if i == 0:
-                regroup_weights_vector(6)
-                regroup_weights_vector(7)
-            if i < BANKS:
-                exponentials(i)
-            if n == 1 and i + 1 < BANKS:
-                shift_scale(i + 1)
-            if n == 0 and 1 <= j < BANKS // PAIR:
-                copy_values(j - 1)
-            if i in (5, 7):
-                regroup_values(nc.scalar.copy, BANKS - PAIR + i // 7)
-            if n == 1 and i < 4:
-                copy_tokens(PACK + i)
-            if n == 0 and i < 4:
-                transpose_tokens(PACK + i)
-            if n == 1 and j < BANKS // PAIR - 1:
-                flip_values(j)
-            if n == 0 and i + 3 < BANKS:
-                project(i + 3)
-            if n == 1 and 1 <= j < BANKS // PAIR:
-                normalise(i - 3, PAIR)
-            if i + 2 < BANKS:
-                maxima(i + 2)
-            if n == 1 and 1 <= j < BANKS // PAIR:
-                quantise_values(i - 3, PAIR)
-            if n == 0 and 1 <= j < BANKS // PAIR:
-                invert_sums(i - 2, PAIR)
-            if i == LAST:
-                invert_sums(LAST - 1, 1)
-                quantise_values(BANKS - PAIR, PAIR)
-            if i == 0:
-                quantise_weights(5, 1)
-            if i == 2:
-                quantise_weights(6, 2)
-            if n == 0 and i < 4:
-                copy_tokens(PACK + i)
-            if i == BANKS:
-                normalise(LAST - 1, 1)
-                invert_sums(LAST, 1)
-            if n == 0 and 2 <= j <= BANKS // PAIR:
-                quantise_probabilities(i - 4, PAIR)
-            if i == BANKS + 1:
-                normalise(LAST, 1)
-            if 17 <= i <= 18:
-                quantise_probabilities(i - 3, 1)
-                summarise(i - 3, 1)
-            if n == 0 and 3 <= j < BANKS // PAIR + 3 - 1:
+        regroup_weights_vector(6)
+        project(3)
+        transpose_tokens(5)
+        transpose_tokens(6)
+        quantise_weights(5, 1)
+        quantise_tokens(4, 1)
+        maxima(2)
+        maxima(3)
+        regroup_weights_vector(7)
+        quantise_weights(6, 1)
+        PAIRS = BANKS // PAIR
+        for j in range(PAIRS):
+            i = PAIR * j
+            exponentials(i)
+            exponentials(i + 1)
+            if j == 0:
+                copy_tokens(5)
+            if i + 4 < BANKS:
+                project(i + 4)
+                project(i + 5)
+            if j == 0:
+                transpose_tokens(7)
+            if j >= 2:
+                summarise(i - 4, PAIR)
+            if j + 1 < PAIRS:
+                shift_scale(j + 1)
+            if j < 2:
+                copy_tokens(6 + j)
+            if j < PAIRS - 1:
+                flip_values(j + 1)
+            if j == 0:
+                regroup_values(0)
+                regroup_values(1)
+            if j >= 1:
+                copy_values(j)
+            if j >= 3:
                 store(i - 6, PAIR)
-            if 18 <= i <= 19:
-                store(i - 4, 1)
+            invert_sums(i, PAIR if j < PAIRS - 1 else 1)
+            if j >= 1:
+                quantise_probabilities(i - 2, PAIR)
+            if i + 4 < BANKS:
+                maxima(i + 4)
+                maxima(i + 5)
+            if j == 0:
+                quantise_tokens(5, 2)
+                quantise_weights(7, 1)
+            if j in (0, 1, 2, 3, 4, 5):
+                normalise(nc.gpsimd, i, DH // 2, DH // 2)
+                normalise(nc.vector, i, 0, DH // 2)
+            else:
+                normalise(nc.vector, i, 0, DH)
+            if j < PAIRS - 1:
+                normalise(nc.vector, i + 1, 0, DH)
+            else:
+                invert_sums(i + 1, 1)
+            if j == 1:
+                quantise_tokens(7, 1)
+            quantise_values(i, PAIR)
+        summarise(12, PAIR)
+        store(10, PAIR)
+        store(12, PAIR)
+        normalise(nc.vector, 15, 0, DH)
+        quantise_probabilities(14, 1)
+        summarise(14, 1)
+        quantise_probabilities(15, 1)
+        summarise(15, 1)
+        store(14, 1)
+        store(15, 1)

@@ -77,16 +77,16 @@ def tile_mhla2_pa_kernel(tc, x_k, W_K, v_heads, out):
         load_weights(4, 1)
         load_weights(2, 1)
         load_weights(3, 1)
+        load_weights(7, 1)
         load_weights(5, 1)
         load_tokens(1, 0)
-        load_weights(6, 2)
+        load_weights(6, 1)
         load_tokens(1, 1)
         load_tokens(1, 2)
         load_values(0, 0, 4)
         load_tokens(1, 3)
         load_values(0, 4, 4)
         load_values(1, 0, 8)
-
 
         identity = keep.tile([P, P], F32)
         make_identity(nc, identity[:])
@@ -135,6 +135,25 @@ def tile_mhla2_pa_kernel(tc, x_k, W_K, v_heads, out):
                     in_=w_raw[:, c].rearrange("p j (c i) -> p c j i", i=4),
                 )
 
+        def regroup_weights_gpsimd(h, g, slot):
+            nc.gpsimd.tensor_scalar(
+                out=w_grouped[:, slot],
+                in0=w_raw[:, h * G + g].rearrange("p j d -> p d j"),
+                scalar1=1.0,
+                scalar2=0.0,
+                op0=ALU.mult,
+                op1=ALU.add,
+            )
+            w_slots[h, g] = slot
+
+        def quantise_slab(h, g):
+            c = h * G + g
+            nc.vector.quantize_mx(
+                out=w_codes[:, c].bitcast(FP8X4),
+                scales=w_scales[:, c],
+                in_=w_grouped[:, w_slots[h, g]].rearrange("p d j -> p (d j)"),
+            )
+
         def quantise_weights(h0, heads):
             slabs = slice(h0 * G, (h0 + heads) * G)
             nc.vector.quantize_mx(
@@ -174,6 +193,7 @@ def tile_mhla2_pa_kernel(tc, x_k, W_K, v_heads, out):
 
         k_banks, row_maxes, shifts, exps, row_sums, inv_sums, p_groupeds, o_banks = {}, {}, {}, {}, {}, {}, {}, {}
         v_flipped = {}
+        w_slots = {}
 
         def project(i):
             b, h = divmod(i, H)
@@ -289,6 +309,7 @@ def tile_mhla2_pa_kernel(tc, x_k, W_K, v_heads, out):
         transpose_tokens(4)
         quantise_weights(4, 1)
         quantise_weights(2, 1)
+        regroup_weights_gpsimd(7, 0, 2 * G)
         maxima(0)
         maxima(1)
         shift_scale(0)
@@ -301,9 +322,9 @@ def tile_mhla2_pa_kernel(tc, x_k, W_K, v_heads, out):
         transpose_tokens(6)
         quantise_weights(5, 1)
         quantise_tokens(4, 1)
+        regroup_weights_gpsimd(7, 1, 5 * G)
         maxima(2)
         maxima(3)
-        regroup_weights_vector(7)
         quantise_weights(6, 1)
         PAIRS = BANKS // PAIR
         for j in range(PAIRS):
@@ -340,7 +361,8 @@ def tile_mhla2_pa_kernel(tc, x_k, W_K, v_heads, out):
                 maxima(i + 5)
             if j == 0:
                 quantise_tokens(5, 2)
-                quantise_weights(7, 1)
+                quantise_slab(7, 0)
+                quantise_slab(7, 1)
             if j in (0, 1, 2, 3, 4, 5):
                 normalise(nc.gpsimd, i, DH // 2, DH // 2)
                 normalise(nc.vector, i, 0, DH // 2)

@@ -30,6 +30,7 @@ def tile_mhla2_pa_kernel(tc, x_k, W_K, v_heads, out):
     with ExitStack() as ctx:
         keep = ctx.enter_context(tc.tile_pool(name="keep", bufs=1))
         ring = ctx.enter_context(tc.tile_pool(name="ring", bufs=4))
+        results = ctx.enter_context(tc.tile_pool(name="results", bufs=8))
         psum_x = ctx.enter_context(tc.psum_pool(name="psum_x", bufs=2))
         psum_k = ctx.enter_context(tc.psum_pool(name="psum_k", bufs=4))
         psum_o = ctx.enter_context(tc.psum_pool(name="psum_o", bufs=2))
@@ -283,7 +284,7 @@ def tile_mhla2_pa_kernel(tc, x_k, W_K, v_heads, out):
         def store(i0, n):
             j, n0 = divmod(i0, PAIR)
             b, h0 = divmod(i0, H)
-            o_sb = ring.tile([P, PAIR, DH], F32, name="o_sb")
+            o_sb = results.tile([P, PAIR, DH], F32, name="o_sb")
             nc.scalar.copy(out=o_sb[:, :n], in_=o_banks[j][:, n0 : n0 + n])
             nc.sync.dma_start(
                 out=out[b, h0 : h0 + n].rearrange("h d e -> d h e"), in_=o_sb[:, :n]
@@ -321,11 +322,11 @@ def tile_mhla2_pa_kernel(tc, x_k, W_K, v_heads, out):
         transpose_tokens(5)
         transpose_tokens(6)
         quantise_weights(5, 1)
-        quantise_tokens(4, 1)
         regroup_weights_gpsimd(7, 1, 5 * G)
         maxima(2)
         maxima(3)
         quantise_weights(6, 1)
+        quantise_tokens(4, 1)
         PAIRS = BANKS // PAIR
         for j in range(PAIRS):
             i = PAIR * j
@@ -354,8 +355,10 @@ def tile_mhla2_pa_kernel(tc, x_k, W_K, v_heads, out):
             if j >= 3:
                 store(i - 6, PAIR)
             invert_sums(i, PAIR if j < PAIRS - 1 else 1)
-            if j >= 1:
+            if 1 <= j < PAIRS - 1:
                 quantise_probabilities(i - 2, PAIR)
+            if j == PAIRS - 1:
+                quantise_values(i - 2, PAIR)
             if i + 4 < BANKS:
                 maxima(i + 4)
                 maxima(i + 5)
@@ -364,22 +367,24 @@ def tile_mhla2_pa_kernel(tc, x_k, W_K, v_heads, out):
                 quantise_slab(7, 0)
                 quantise_slab(7, 1)
             if j in (0, 1, 2, 3, 4, 5):
-                normalise(nc.gpsimd, i, DH // 2, DH // 2)
-                normalise(nc.vector, i, 0, DH // 2)
+                normalise(nc.gpsimd, i, DH - 80, 80)
+                normalise(nc.vector, i, 0, DH - 80)
             else:
                 normalise(nc.vector, i, 0, DH)
             if j < PAIRS - 1:
                 normalise(nc.vector, i + 1, 0, DH)
             else:
                 invert_sums(i + 1, 1)
+                quantise_probabilities(i - 2, PAIR)
+                normalise(nc.vector, i + 1, 0, DH)
+                quantise_probabilities(i, 1)
             if j == 1:
                 quantise_tokens(7, 1)
-            quantise_values(i, PAIR)
+            if j != PAIRS - 2:
+                quantise_values(i, PAIR)
         summarise(12, PAIR)
         store(10, PAIR)
         store(12, PAIR)
-        normalise(nc.vector, 15, 0, DH)
-        quantise_probabilities(14, 1)
         summarise(14, 1)
         quantise_probabilities(15, 1)
         summarise(15, 1)

@@ -367,8 +367,8 @@ def tile_mhla2_pa_kernel(tc, x_k, W_K, v_heads, out):
                 quantise_slab(7, 0)
                 quantise_slab(7, 1)
             if j in (0, 1, 2, 3, 4, 5):
-                normalise(nc.gpsimd, i, DH - 80, 80)
-                normalise(nc.vector, i, 0, DH - 80)
+                normalise(nc.gpsimd, i, DH - 96, 96)
+                normalise(nc.vector, i, 0, DH - 96)
             else:
                 normalise(nc.vector, i, 0, DH)
             if j < PAIRS - 1:

from contextlib import ExitStack

import concourse.mybir as mybir
from concourse.masks import make_identity

F32 = mybir.dt.float32
BF16 = mybir.dt.bfloat16
U32 = mybir.dt.uint32
U8 = mybir.dt.uint8
FP8X4 = mybir.dt.float8_e4m3fn_x4
ACT = mybir.ActivationFunctionType
ALU = mybir.AluOpType
AXIS = mybir.AxisListType

B, S, D, H, DH = 2, 512, 1024, 8, 128
P = 128
PACK = 4
K_PASS = P * PACK
G = D // K_PASS
TOKEN_TILES = B * S // P
BANKS = B * H
PAIR = 2
SOFTMAX_SCALE = DH ** -0.25

FLOPS = 2 * B * H * S * D * DH + 2 * B * H * S * DH * DH


def tile_mhla2_pa_kernel(tc, x_k, W_K, v_heads, out):
    nc = tc.nc
    with ExitStack() as ctx:
        keep = ctx.enter_context(tc.tile_pool(name="keep", bufs=1))
        ring = ctx.enter_context(tc.tile_pool(name="ring", bufs=4))
        results = ctx.enter_context(tc.tile_pool(name="results", bufs=8))
        psum_x = ctx.enter_context(tc.psum_pool(name="psum_x", bufs=2))
        psum_k = ctx.enter_context(tc.psum_pool(name="psum_k", bufs=4))
        psum_o = ctx.enter_context(tc.psum_pool(name="psum_o", bufs=2))
        ctx.enter_context(tc.manual_schedule())

        x_raw = keep.tile([P, TOKEN_TILES, D], BF16)
        x_grouped = keep.tile([P, TOKEN_TILES, G, P * PACK], BF16, align_bytes=64)
        x_codes = keep.tile([P, TOKEN_TILES, G, P], U32, align_bytes=64)
        x_scales = keep.tile([P, TOKEN_TILES, G, P], U8, align_bytes=64)
        w_raw = keep.tile([P, H * G, PACK, DH], BF16)
        w_grouped = keep.tile([P, H * G, DH, PACK], BF16, align_bytes=64)
        w_codes = keep.tile([P, H * G, DH], U32, align_bytes=64)
        w_scales = keep.tile([P, H * G, DH], U8, align_bytes=64)
        v_raw = keep.tile([P, BANKS, PACK, DH], BF16)
        v_grouped = keep.tile([P, BANKS, DH, PACK], BF16, align_bytes=64)
        v_codes = keep.tile([P, BANKS, DH], U32, align_bytes=64)
        v_scales = keep.tile([P, BANKS, DH], U8, align_bytes=64)
        p_codes = keep.tile([P, BANKS, DH], U32, align_bytes=64)
        p_scales = keep.tile([P, BANKS, DH], U8, align_bytes=64)

        def load_weights(h0, heads):
            nc.sync.dma_start(
                out=w_raw[:, h0 * G : (h0 + heads) * G],
                in_=W_K[h0 : h0 + heads].rearrange("h (g p j) d -> p (h g) j d", g=G, j=PACK),
            )

        def load_tokens(b, t):
            nc.sync.dma_start(
                out=x_raw[:, PACK * b + t, :],
                in_=x_k[b].rearrange("(p t) f -> p t f", t=PACK)[:, t, :],
            )

        def load_values(b, h0, heads):
            nc.sync.dma_start(
                out=v_raw[:, H * b + h0 : H * b + h0 + heads],
                in_=v_heads[b, h0 : h0 + heads].rearrange("h (p t) e -> p h t e", t=PACK),
            )

        load_tokens(0, 0)
        load_tokens(0, 1)
        load_weights(0, 1)
        load_tokens(0, 2)
        load_tokens(0, 3)
        load_weights(1, 1)
        load_weights(4, 1)
        load_weights(2, 1)
        load_weights(3, 1)
        load_weights(7, 1)
        load_weights(5, 1)
        load_tokens(1, 0)
        load_weights(6, 1)
        load_tokens(1, 1)
        load_tokens(1, 2)
        load_values(0, 0, 4)
        load_tokens(1, 3)
        load_values(0, 4, 4)
        load_values(1, 0, 8)

        identity = keep.tile([P, P], F32)
        make_identity(nc, identity[:])
        identity_bf16 = keep.tile([P, P], BF16)
        make_identity(nc, identity_bf16[:])

        warm = keep.tile([P, 1], F32)
        nc.vector.memset(warm[:], 0.0)
        nc.scalar.activation(out=warm[:], in_=warm[:], func=ACT.Exp)

        x_flipped = {}

        def transpose_tokens(tt):
            words = x_raw[:, tt, :].bitcast(F32).rearrange("p (g q u) -> p g u q", g=G, u=2)
            flipped = psum_x.tile([P, G, 2, P], F32, name="flipped")
            for g in range(G):
                for u in range(2):
                    nc.tensor.transpose(flipped[:, g, u, :], words[:, g, u, :], identity[:])
            x_flipped[tt] = flipped

        def copy_tokens(tt):
            flipped = x_flipped[tt]
            nc.scalar.copy(
                out=x_grouped[:, tt].bitcast(F32).rearrange("p g (n u) -> p g n u", u=2),
                in_=flipped[:].rearrange("p g u n -> p g n u"),
            )

        def quantise_tokens(tt, n):
            nc.vector.quantize_mx(
                out=x_codes[:, tt : tt + n].rearrange("p s g n -> p (s g n)").bitcast(FP8X4),
                scales=x_scales[:, tt : tt + n].rearrange("p s g n -> p (s g n)"),
                in_=x_grouped[:, tt : tt + n].rearrange("p s g c -> p (s g c)"),
            )

        def regroup_weights_vector(h):
            slabs = slice(h * G, (h + 1) * G)
            nc.vector.tensor_copy(
                out=w_grouped[:, slabs].rearrange("p s (c i) j -> p s c j i", i=8),
                in_=w_raw[:, slabs].rearrange("p s j (c i) -> p s c j i", i=8),
            )

        def regroup_weights_scalar(h):
            for c in range(h * G, (h + 1) * G):
                nc.scalar.copy(
                    out=w_grouped[:, c].rearrange("p (c i) j -> p c j i", i=4),
                    in_=w_raw[:, c].rearrange("p j (c i) -> p c j i", i=4),
                )

        def regroup_weights_gpsimd(h, g, slot):
            nc.gpsimd.tensor_scalar(
                out=w_grouped[:, slot],
                in0=w_raw[:, h * G + g].rearrange("p j d -> p d j"),
                scalar1=1.0,
                scalar2=0.0,
                op0=ALU.mult,
                op1=ALU.add,
            )
            w_slots[h, g] = slot

        def quantise_slab(h, g):
            c = h * G + g
            nc.vector.quantize_mx(
                out=w_codes[:, c].bitcast(FP8X4),
                scales=w_scales[:, c],
                in_=w_grouped[:, w_slots[h, g]].rearrange("p d j -> p (d j)"),
            )

        def quantise_weights(h0, heads):
            slabs = slice(h0 * G, (h0 + heads) * G)
            nc.vector.quantize_mx(
                out=w_codes[:, slabs].rearrange("p s d -> p (s d)").bitcast(FP8X4),
                scales=w_scales[:, slabs].rearrange("p s d -> p (s d)"),
                in_=w_grouped[:, slabs].rearrange("p s d j -> p (s d j)"),
            )

        def flip_values(j):
            flipped = psum_x.tile([P, PAIR, DH, PACK], BF16, name="flipped")
            for n in range(PAIR):
                nc.tensor.matmul(
                    flipped[:, n],
                    lhsT=identity_bf16[:],
                    rhs=v_raw[:, PAIR * j + n].rearrange("p j d -> p d j"),
                    start=True,
                    stop=True,
                )
            v_flipped[j] = flipped

        def copy_values(j):
            nc.scalar.copy(out=v_grouped[:, PAIR * j : PAIR * (j + 1)], in_=v_flipped[j][:])

        def regroup_values(i):
            nc.scalar.copy(
                out=v_grouped[:, i].rearrange("p (c i) j -> p c j i", i=4),
                in_=v_raw[:, i].rearrange("p j (c i) -> p c j i", i=4),
            )

        def quantise_values(i0, n):
            banks = slice(i0, i0 + n)
            nc.vector.quantize_mx(
                out=v_codes[:, banks].rearrange("p s d -> p (s d)").bitcast(FP8X4),
                scales=v_scales[:, banks].rearrange("p s d -> p (s d)"),
                in_=v_grouped[:, banks].rearrange("p s d j -> p (s d j)"),
            )

        k_banks, row_maxes, shifts, exps, row_sums, inv_sums, p_groupeds, o_banks = {}, {}, {}, {}, {}, {}, {}, {}
        v_flipped = {}
        w_slots = {}

        def project(i):
            b, h = divmod(i, H)
            k_banks[i] = psum_k.tile([P, PACK, DH], F32, name="k_bank")
            for t in range(PACK):
                for g in range(G):
                    nc.tensor.matmul_mx(
                        out=k_banks[i][:, t, :],
                        lhsT=x_codes[:, PACK * b + t, g, :].bitcast(FP8X4),
                        lhsT_scale=x_scales[:, PACK * b + t, g, :],
                        rhs=w_codes[:, h * G + g, :].bitcast(FP8X4),
                        rhs_scale=w_scales[:, h * G + g, :],
                        start=(g == 0),
                        stop=(g == G - 1),
                    )

        def maxima(i):
            j, n = divmod(i, PAIR)
            if n == 0:
                row_maxes[j] = ring.tile([P, PAIR, PACK], F32, name="row_max")
            nc.vector.tensor_reduce(
                out=row_maxes[j][:, n], in_=k_banks[i][:], axis=AXIS.X, op=ALU.max
            )

        def shift_scale(j):
            shifts[j] = ring.tile([P, PAIR, PACK], F32, name="shift")
            nc.scalar.mul(out=shifts[j][:], in_=row_maxes[j][:], mul=-SOFTMAX_SCALE)

        def exponentials(i):
            j, n = divmod(i, PAIR)
            if n == 0:
                exps[j] = ring.tile([P, PAIR, PACK, DH], F32, name="e")
                row_sums[j] = ring.tile([P, PAIR, PACK], F32, name="row_sum")
            for t in range(PACK):
                nc.scalar.activation(
                    out=exps[j][:, n, t, :],
                    in_=k_banks[i][:, t, :],
                    func=ACT.Exp,
                    bias=shifts[j][:, n, t : t + 1],
                    scale=SOFTMAX_SCALE,
                    accum_out=row_sums[j][:, n, t : t + 1],
                )

        def invert_sums(i0, n):
            j, n0 = divmod(i0, PAIR)
            if n0 == 0:
                inv_sums[j] = ring.tile([P, PAIR, PACK], F32, name="inv_sum")
                p_groupeds[j] = ring.tile([P, PAIR, DH, PACK], BF16, name="p_grouped", align_bytes=64)
            nc.vector.reciprocal(
                out=inv_sums[j][:, n0 : n0 + n], in_=row_sums[j][:, n0 : n0 + n]
            )

        def normalise(engine, i, d0, width):
            j, n = divmod(i, PAIR)
            features = slice(d0, d0 + width)
            engine.tensor_tensor(
                out=p_groupeds[j][:, n, features].rearrange("p (c i) t -> p c t i", i=4),
                in0=exps[j][:, n, :, features].rearrange("p t (c i) -> p c t i", i=4),
                in1=inv_sums[j][:, n].unsqueeze(1).unsqueeze(3).to_broadcast([P, width // 4, PACK, 4]),
                op=ALU.mult,
            )

        def quantise_probabilities(i0, n):
            j, n0 = divmod(i0, PAIR)
            banks = slice(i0, i0 + n)
            nc.vector.quantize_mx(
                out=p_codes[:, banks].rearrange("p n d -> p (n d)").bitcast(FP8X4),
                scales=p_scales[:, banks].rearrange("p n d -> p (n d)"),
                in_=p_groupeds[j][:, n0 : n0 + n].rearrange("p n d t -> p (n d t)"),
            )

        def summarise(i0, n):
            j, n0 = divmod(i0, PAIR)
            if n0 == 0:
                o_banks[j] = psum_o.tile([P, PAIR, DH], F32, name="o_bank")
            for i in range(i0, i0 + n):
                nc.tensor.matmul_mx(
                    out=o_banks[j][:, i % PAIR, :],
                    lhsT=p_codes[:, i, :].bitcast(FP8X4),
                    lhsT_scale=p_scales[:, i, :],
                    rhs=v_codes[:, i, :].bitcast(FP8X4),
                    rhs_scale=v_scales[:, i, :],
                    start=True,
                    stop=True,
                )

        def store(i0, n):
            j, n0 = divmod(i0, PAIR)
            b, h0 = divmod(i0, H)
            o_sb = results.tile([P, PAIR, DH], F32, name="o_sb")
            nc.scalar.copy(out=o_sb[:, :n], in_=o_banks[j][:, n0 : n0 + n])
            nc.sync.dma_start(
                out=out[b, h0 : h0 + n].rearrange("h d e -> d h e"), in_=o_sb[:, :n]
            )

        regroup_weights_vector(0)
        for t in range(PACK):
            transpose_tokens(t)
            copy_tokens(t)
        quantise_tokens(0, 1)
        quantise_weights(0, 1)
        quantise_tokens(1, 1)
        regroup_weights_scalar(4)
        regroup_weights_vector(1)
        regroup_weights_scalar(3)
        quantise_tokens(2, 1)
        regroup_weights_scalar(5)
        quantise_weights(1, 1)
        quantise_tokens(3, 1)
        regroup_weights_vector(2)
        project(0)
        project(1)
        transpose_tokens(4)
        quantise_weights(4, 1)
        quantise_weights(2, 1)
        regroup_weights_gpsimd(7, 0, 2 * G)
        maxima(0)
        maxima(1)
        shift_scale(0)
        copy_tokens(4)
        project(2)
        quantise_weights(3, 1)
        regroup_weights_vector(6)
        project(3)
        transpose_tokens(5)
        transpose_tokens(6)
        quantise_weights(5, 1)
        regroup_weights_gpsimd(7, 1, 5 * G)
        maxima(2)
        maxima(3)
        quantise_weights(6, 1)
        quantise_tokens(4, 1)
        PAIRS = BANKS // PAIR
        for j in range(PAIRS):
            i = PAIR * j
            exponentials(i)
            exponentials(i + 1)
            if j == 0:
                copy_tokens(5)
            if i + 4 < BANKS:
                project(i + 4)
                project(i + 5)
            if j == 0:
                transpose_tokens(7)
            if j >= 2:
                summarise(i - 4, PAIR)
            if j + 1 < PAIRS:
                shift_scale(j + 1)
            if j < 2:
                copy_tokens(6 + j)
            if j < PAIRS - 1:
                flip_values(j + 1)
            if j == 0:
                regroup_values(0)
                regroup_values(1)
            if j >= 1:
                copy_values(j)
            if j >= 3:
                store(i - 6, PAIR)
            invert_sums(i, PAIR if j < PAIRS - 1 else 1)
            if 1 <= j < PAIRS - 1:
                quantise_probabilities(i - 2, PAIR)
            if j == PAIRS - 1:
                quantise_values(i - 2, PAIR)
            if i + 4 < BANKS:
                maxima(i + 4)
                maxima(i + 5)
            if j == 0:
                quantise_tokens(5, 2)
                quantise_slab(7, 0)
                quantise_slab(7, 1)
            if j in (0, 1, 2, 3, 4, 5):
                normalise(nc.gpsimd, i, DH - 96, 96)
                normalise(nc.vector, i, 0, DH - 96)
            else:
                normalise(nc.vector, i, 0, DH)
            if j < PAIRS - 1:
                normalise(nc.vector, i + 1, 0, DH)
            else:
                invert_sums(i + 1, 1)
                quantise_probabilities(i - 2, PAIR)
                normalise(nc.vector, i + 1, 0, DH)
                quantise_probabilities(i, 1)
            if j == 1:
                quantise_tokens(7, 1)
            if j != PAIRS - 2:
                quantise_values(i, PAIR)
        summarise(12, PAIR)
        store(10, PAIR)
        store(12, PAIR)
        summarise(14, 1)
        quantise_probabilities(15, 1)
        summarise(15, 1)
        store(14, 1)
        store(15, 1)
